import numpy as np
import ml_dtypes


def mxq(x, axis, fmt="e4m3"):
    dtype, down = {"e4m3": (ml_dtypes.float8_e4m3fn, 7), "e5m2": (ml_dtypes.float8_e5m2, 14)}[fmt]
    v = np.moveaxis(np.asarray(x, np.float32).astype(ml_dtypes.bfloat16).astype(np.float64), axis, -1)
    blocks = v.reshape(v.shape[:-1] + (-1, 32))
    amax = np.abs(blocks).max(-1, keepdims=True)
    byte = np.maximum(np.where(amax > 0, np.frexp(amax)[1] - 1 + 127, 0) - down, 1)
    scale = np.exp2(byte - 127.0)
    codes = (blocks / scale).astype(np.float32).astype(dtype).astype(np.float64)
    return np.moveaxis((codes * scale).reshape(v.shape), -1, axis)


WIDE = False


def mx_kscale(k):
    if not WIDE:
        return np.ones(k)
    levels = np.array([10, -10, 5, -5, 0])
    a = np.random.permutation(np.resize(levels, k // 512 * 4)).reshape(k // 512, 4)
    idx = np.arange(k)
    return np.exp2(a[idx // 512, idx % 128 // 32])


BF16 = ml_dtypes.bfloat16


def bf(x):
    return np.asarray(x, np.float32).astype(BF16)


def f64(x):
    return np.asarray(x).astype(np.float64)


E2M1 = np.array([0.0, 0.5, 1.0, 1.5, 2.0, 3.0, 4.0, 6.0, -0.0, -0.5, -1.0, -1.5, -2.0, -3.0, -4.0, -6.0])


def pack_weight(w, fmt):
    k, n = w.shape
    w = f64(bf(w)).reshape(k // 32, 32, n)
    amax = np.abs(w).max(1)
    if fmt == "e4m3":
        byte = np.frexp(amax)[1] - 1 + 127 - 7
    else:
        mant, ex = np.frexp(amax / 6.0)
        byte = np.where(mant > 0.5, ex, ex - 1) + 127
    byte = np.clip(np.where(amax > 0, byte, 1), 1, 254)
    scaled = (w * np.exp2(127.0 - byte)[:, None, :]).reshape(k, n).astype(np.float32)
    by_word = np.ascontiguousarray(scaled.reshape(k // 512, 128, 4, n).transpose(0, 1, 3, 2))
    if fmt == "e4m3":
        words = by_word.astype(ml_dtypes.float8_e4m3fn).view(np.uint8)
    else:
        c = by_word.astype(ml_dtypes.float4_e2m1fn).view(np.uint8) & 0xF
        words = c[..., 0::2] | (c[..., 1::2] << 4)
    return np.ascontiguousarray(words), np.ascontiguousarray(byte.astype(np.uint8).reshape(k // 512, 16, n))


def unpack_weight(words, scales, fmt):
    g, p, n, _ = words.shape
    if fmt == "e4m3":
        vals = np.ascontiguousarray(words).view(ml_dtypes.float8_e4m3fn).astype(np.float64)
    else:
        nib = np.empty((g, p, n, 4), np.uint8)
        nib[..., 0::2] = words & 0xF
        nib[..., 1::2] = words >> 4
        vals = E2M1[nib]
    vals = vals * np.repeat(np.exp2(scales.astype(np.float64) - 127.0), 8, axis=1)[..., None]
    return vals.transpose(0, 1, 3, 2).reshape(g * 512, n)


C_COUNT, NC, ROW, COL = 8, 48, 512, 512


def setup_inputs():
    s = mx_kscale(ROW)
    Pb = bf(np.random.standard_normal((C_COUNT, ROW, ROW)) * 1.25 / np.sqrt(ROW))
    Ev = bf(np.random.standard_normal((C_COUNT, ROW, ROW)) * s)
    stack = np.random.standard_normal((C_COUNT, ROW, ROW)) / np.sqrt(ROW) / s[:, None]
    words, scales = pack_weight(stack.reshape(-1, ROW), "e4m3")
    feat = bf(np.random.standard_normal((C_COUNT, ROW, COL)))
    return {"Pb": Pb, "Ev": Ev, "W_pie_words": words, "W_pie_scales": scales, "feat": feat}


def reference(Pb, Ev, W_pie_words, W_pie_scales, feat):
    W = unpack_weight(W_pie_words, W_pie_scales, "e4m3").reshape(C_COUNT, ROW, ROW)
    T = mxq(f64(Ev), 2, "e4m3") @ W
    d = (f64(Pb) * T.transpose(0, 2, 1)).sum(-1)
    return 0.3 * d[:, :, None] * f64(feat) + f64(feat)

@@ -1,0 +1,114 @@
+from contextlib import ExitStack
+
+import concourse.mybir as mybir
+from concourse.masks import make_identity
+
+F32 = mybir.dt.float32
+BF16 = mybir.dt.bfloat16
+I32 = mybir.dt.int32
+U32 = mybir.dt.uint32
+U8 = mybir.dt.uint8
+FP8X4 = mybir.dt.float8_e4m3fn_x4
+MULT = mybir.AluOpType.mult
+COPY = mybir.ActivationFunctionType.Copy
+
+P = 128
+PACK = 4
+C = 8
+ROW = 512
+TILES = ROW // P
+PAIRS = ROW // 2
+QUADRANTS = 4
+GAIN = 0.3
+
+FLOPS = C * (2 * ROW * ROW * ROW + 2 * ROW * ROW + 3 * ROW * ROW)
+
+
+def tile_generator_pa_e_kernel(tc, Pb, Ev, W_pie_words, W_pie_scales, feat, out):
+    nc = tc.nc
+    with ExitStack() as stack:
+        const = stack.enter_context(tc.tile_pool(name="const", bufs=1))
+        loads = stack.enter_context(tc.tile_pool(name="loads", bufs=C))
+        work = stack.enter_context(tc.tile_pool(name="work", bufs=2))
+        results = stack.enter_context(tc.tile_pool(name="results", bufs=C))
+        psum_flip = stack.enter_context(tc.psum_pool(name="psum_flip", bufs=4))
+        psum_tt = stack.enter_context(tc.psum_pool(name="psum_tt", bufs=4))
+
+        ident = const.tile([P, P], F32)
+        make_identity(nc, ident[:])
+
+        w_codes = const.tile([P, C, ROW], U32, align_bytes=64)
+        w_scales = const.tile([P, C, ROW], U8, align_bytes=64)
+        nc.vector.memset(w_scales[:].rearrange("p c n -> p (c n)").bitcast(I32), 0)
+
+        ev_rows, pb_rows, feat_rows = [], [], []
+        for c in range(C):
+            ev_c = loads.tile([P, TILES, ROW], BF16, name="ev_c", tag="ev")
+            nc.sync.dma_start(out=ev_c[:], in_=Ev[c].rearrange("(p r) k -> p r k", r=TILES))
+            ev_rows.append(ev_c)
+            if c == 0:
+                for quad in range(QUADRANTS):
+                    nc.sync.dma_start(
+                        out=w_scales[32 * quad : 32 * quad + 4, :, :].bitcast(I32),
+                        in_=W_pie_scales[:, 4 * quad : 4 * quad + 4, :].rearrange("c r n -> r c n").bitcast(I32),
+                    )
+            nc.sync.dma_start(
+                out=w_codes[:, c, :].bitcast(I32),
+                in_=W_pie_words[c].rearrange("p n t -> p (n t)").bitcast(I32),
+            )
+            pb_c = loads.tile([P, TILES, ROW], BF16, name="pb_c", tag="pb")
+            nc.sync.dma_start(out=pb_c[:], in_=Pb[c].rearrange("(s m) j -> m s j", m=P))
+            pb_rows.append(pb_c)
+            feat_c = loads.tile([P, TILES, ROW], BF16, name="feat_c", tag="feat")
+            nc.sync.dma_start(out=feat_c[:], in_=feat[c].rearrange("(s m) n -> m s n", m=P))
+            feat_rows.append(feat_c)
+
+        for c in range(C):
+            ev_pairs = ev_rows[c][:].rearrange("p r k -> p (r k)").bitcast(F32)
+            ev_kfirst = work.tile([P, ROW * PACK], BF16, align_bytes=64)
+            kfirst_pairs = ev_kfirst[:].bitcast(F32).rearrange("q (p half a) -> q p half a", half=2, a=4)
+            for half in range(2):
+                flipped = psum_flip.tile([P, 4, P], F32)
+                for a in range(4):
+                    r, u = 2 * half + a // 2, a % 2
+                    nc.tensor.transpose(
+                        flipped[:, a, :], ev_pairs[:, PAIRS * r + u : PAIRS * (r + 1) : 2], ident[:]
+                    )
+                nc.scalar.copy(out=kfirst_pairs[:, :, half, :], in_=flipped[:].rearrange("q a p -> q p a"))
+
+            ev_codes = work.tile([P, ROW], U32, align_bytes=64)
+            ev_scales = work.tile([P, ROW], U8, align_bytes=64)
+            nc.vector.quantize_mx(out=ev_codes[:].bitcast(FP8X4), scales=ev_scales[:], in_=ev_kfirst[:])
+
+            gain_d = work.tile([P, TILES], F32)
+            for s in range(TILES):
+                i_cols = slice(P * s, P * (s + 1))
+                tt = psum_tt.tile([P, ROW], F32)
+                nc.tensor.matmul_mx(
+                    out=tt[:],
+                    lhsT=w_codes[:, c, i_cols].bitcast(FP8X4),
+                    lhsT_scale=w_scales[:, c, i_cols],
+                    rhs=ev_codes[:].bitcast(FP8X4),
+                    rhs_scale=ev_scales[:],
+                    start=True,
+                    stop=True,
+                )
+                products = work.tile([P, ROW], F32)
+                nc.vector.scalar_tensor_tensor(
+                    out=products[:],
+                    in0=tt[:],
+                    scalar=GAIN,
+                    in1=pb_rows[c][:, s, :],
+                    op0=MULT,
+                    op1=MULT,
+                    accum_out=gain_d[:, s : s + 1],
+                )
+
+            factor = work.tile([P, TILES], F32)
+            nc.vector.tensor_scalar_add(out=factor[:], in0=gain_d[:], scalar1=1.0)
+            out_rows = results.tile([P, TILES, ROW], F32)
+            for s in range(TILES):
+                nc.scalar.activation(
+                    out=out_rows[:, s, :], in_=feat_rows[c][:, s, :], func=COPY, scale=factor[:, s : s + 1]
+                )
+            nc.sync.dma_start(out=out[c].rearrange("(s m) n -> m s n", m=P), in_=out_rows[:])

@@ -9,8 +9,10 @@ I32 = mybir.dt.int32
 U32 = mybir.dt.uint32
 U8 = mybir.dt.uint8
 FP8X4 = mybir.dt.float8_e4m3fn_x4
+ADD = mybir.AluOpType.add
 MULT = mybir.AluOpType.mult
 COPY = mybir.ActivationFunctionType.Copy
+ALONG_ROW = mybir.AxisListType.X
 
 P = 128
 PACK = 4
@@ -21,94 +23,130 @@ PAIRS = ROW // 2
 QUADRANTS = 4
 GAIN = 0.3
 
+GROUP = 1
+CHUNKS = C // GROUP
+ROWS_HERE = GROUP * ROW // P
+BLOCKS = P // ROWS_HERE
+
 FLOPS = C * (2 * ROW * ROW * ROW + 2 * ROW * ROW + 3 * ROW * ROW)
 
 
 def tile_generator_pa_e_kernel(tc, Pb, Ev, W_pie_words, W_pie_scales, feat, out):
     nc = tc.nc
+    ev_chunks = Ev.rearrange("(g c) j k -> g (c j) k", c=GROUP)
+    feat_chunks = feat.rearrange("(g c) i n -> g (c i) n", c=GROUP)
+    out_chunks = out.rearrange("(g c) i n -> g (c i) n", c=GROUP)
+
     with ExitStack() as stack:
         const = stack.enter_context(tc.tile_pool(name="const", bufs=1))
-        loads = stack.enter_context(tc.tile_pool(name="loads", bufs=C))
+        chunk_loads = stack.enter_context(tc.tile_pool(name="chunk_loads", bufs=CHUNKS))
+        pb_loads = stack.enter_context(tc.tile_pool(name="pb_loads", bufs=C))
         work = stack.enter_context(tc.tile_pool(name="work", bufs=2))
-        results = stack.enter_context(tc.tile_pool(name="results", bufs=C))
-        psum_flip = stack.enter_context(tc.psum_pool(name="psum_flip", bufs=4))
+        results = stack.enter_context(tc.tile_pool(name="results", bufs=CHUNKS))
+        psum_flip = stack.enter_context(tc.psum_pool(name="psum_flip", bufs=2))
         psum_tt = stack.enter_context(tc.psum_pool(name="psum_tt", bufs=4))
+        psum_moved = stack.enter_context(tc.psum_pool(name="psum_moved", bufs=2))
 
         ident = const.tile([P, P], F32)
         make_identity(nc, ident[:])
+        in_block = const.tile([P, BLOCKS], F32)
+        nc.vector.tensor_reduce(
+            out=in_block[:], in_=ident[:].rearrange("m (b r) -> m b r", r=ROWS_HERE), axis=ALONG_ROW, op=ADD
+        )
+        at_offset = const.tile([P, ROWS_HERE], F32)
+        nc.vector.tensor_reduce(
+            out=at_offset[:], in_=ident[:].rearrange("m (b r) -> m r b", r=ROWS_HERE), axis=ALONG_ROW, op=ADD
+        )
 
         w_codes = const.tile([P, C, ROW], U32, align_bytes=64)
         w_scales = const.tile([P, C, ROW], U8, align_bytes=64)
         nc.vector.memset(w_scales[:].rearrange("p c n -> p (c n)").bitcast(I32), 0)
 
         ev_rows, pb_rows, feat_rows = [], [], []
-        for c in range(C):
-            ev_c = loads.tile([P, TILES, ROW], BF16, name="ev_c", tag="ev")
-            nc.sync.dma_start(out=ev_c[:], in_=Ev[c].rearrange("(p r) k -> p r k", r=TILES))
-            ev_rows.append(ev_c)
-            if c == 0:
+        for g in range(CHUNKS):
+            ev_g = chunk_loads.tile([P, ROWS_HERE, ROW], BF16, name="ev_g", tag="ev")
+            nc.sync.dma_start(out=ev_g[:], in_=ev_chunks[g].rearrange("(p r) k -> p r k", r=ROWS_HERE))
+            ev_rows.append(ev_g)
+            if g == 0:
                 for quad in range(QUADRANTS):
                     nc.sync.dma_start(
                         out=w_scales[32 * quad : 32 * quad + 4, :, :].bitcast(I32),
                         in_=W_pie_scales[:, 4 * quad : 4 * quad + 4, :].rearrange("c r n -> r c n").bitcast(I32),
                     )
-            nc.sync.dma_start(
-                out=w_codes[:, c, :].bitcast(I32),
-                in_=W_pie_words[c].rearrange("p n t -> p (n t)").bitcast(I32),
-            )
-            pb_c = loads.tile([P, TILES, ROW], BF16, name="pb_c", tag="pb")
-            nc.sync.dma_start(out=pb_c[:], in_=Pb[c].rearrange("(s m) j -> m s j", m=P))
-            pb_rows.append(pb_c)
-            feat_c = loads.tile([P, TILES, ROW], BF16, name="feat_c", tag="feat")
-            nc.sync.dma_start(out=feat_c[:], in_=feat[c].rearrange("(s m) n -> m s n", m=P))
-            feat_rows.append(feat_c)
+            for c in range(GROUP * g, GROUP * (g + 1)):
+                nc.sync.dma_start(
+                    out=w_codes[:, c, :].bitcast(I32),
+                    in_=W_pie_words[c].rearrange("p n t -> p (n t)").bitcast(I32),
+                )
+                pb_c = pb_loads.tile([P, TILES, ROW], BF16)
+                nc.sync.dma_start(out=pb_c[:], in_=Pb[c].rearrange("(s m) j -> m s j", m=P))
+                pb_rows.append(pb_c)
+            feat_g = chunk_loads.tile([P, ROWS_HERE, ROW], BF16, name="feat_g", tag="feat")
+            nc.sync.dma_start(out=feat_g[:], in_=feat_chunks[g].rearrange("(p r) n -> p r n", r=ROWS_HERE))
+            feat_rows.append(feat_g)
 
-        for c in range(C):
-            ev_pairs = ev_rows[c][:].rearrange("p r k -> p (r k)").bitcast(F32)
-            ev_kfirst = work.tile([P, ROW * PACK], BF16, align_bytes=64)
-            kfirst_pairs = ev_kfirst[:].bitcast(F32).rearrange("q (p half a) -> q p half a", half=2, a=4)
-            for half in range(2):
+        for g in range(CHUNKS):
+            ev_pairs = ev_rows[g][:].rearrange("p r k -> p (r k)").bitcast(F32)
+            ev_kfirst = work.tile([P, GROUP * ROW * PACK], BF16, align_bytes=64)
+            kfirst_pairs = ev_kfirst[:].bitcast(F32).rearrange("q (p h a) -> q p h a", h=ROWS_HERE // 2, a=4)
+            for h in range(ROWS_HERE // 2):
                 flipped = psum_flip.tile([P, 4, P], F32)
                 for a in range(4):
-                    r, u = 2 * half + a // 2, a % 2
+                    r, u = 2 * h + a // 2, a % 2
                     nc.tensor.transpose(
                         flipped[:, a, :], ev_pairs[:, PAIRS * r + u : PAIRS * (r + 1) : 2], ident[:]
                     )
-                nc.scalar.copy(out=kfirst_pairs[:, :, half, :], in_=flipped[:].rearrange("q a p -> q p a"))
+                nc.scalar.copy(out=kfirst_pairs[:, :, h, :], in_=flipped[:].rearrange("q a p -> q p a"))
 
-            ev_codes = work.tile([P, ROW], U32, align_bytes=64)
-            ev_scales = work.tile([P, ROW], U8, align_bytes=64)
-            nc.vector.quantize_mx(out=ev_codes[:].bitcast(FP8X4), scales=ev_scales[:], in_=ev_kfirst[:])
-
-            gain_d = work.tile([P, TILES], F32)
-            for s in range(TILES):
-                i_cols = slice(P * s, P * (s + 1))
-                tt = psum_tt.tile([P, ROW], F32)
-                nc.tensor.matmul_mx(
-                    out=tt[:],
-                    lhsT=w_codes[:, c, i_cols].bitcast(FP8X4),
-                    lhsT_scale=w_scales[:, c, i_cols],
-                    rhs=ev_codes[:].bitcast(FP8X4),
-                    rhs_scale=ev_scales[:],
-                    start=True,
-                    stop=True,
+            ev_codes = work.tile([P, GROUP, ROW], U32, align_bytes=64)
+            ev_scales = work.tile([P, GROUP, ROW], U8, align_bytes=64)
+            gain_d = work.tile([P, GROUP * TILES], F32)
+            for c in range(GROUP):
+                nc.vector.quantize_mx(
+                    out=ev_codes[:, c, :].bitcast(FP8X4),
+                    scales=ev_scales[:, c, :],
+                    in_=ev_kfirst[:, ROW * PACK * c : ROW * PACK * (c + 1)],
                 )
-                products = work.tile([P, ROW], F32)
-                nc.vector.scalar_tensor_tensor(
-                    out=products[:],
-                    in0=tt[:],
-                    scalar=GAIN,
-                    in1=pb_rows[c][:, s, :],
-                    op0=MULT,
-                    op1=MULT,
-                    accum_out=gain_d[:, s : s + 1],
-                )
+                for s in range(TILES):
+                    i_cols = slice(P * s, P * (s + 1))
+                    tt = psum_tt.tile([P, ROW], F32)
+                    nc.tensor.matmul_mx(
+                        out=tt[:],
+                        lhsT=w_codes[:, GROUP * g + c, i_cols].bitcast(FP8X4),
+                        lhsT_scale=w_scales[:, GROUP * g + c, i_cols],
+                        rhs=ev_codes[:, c, :].bitcast(FP8X4),
+                        rhs_scale=ev_scales[:, c, :],
+                        start=True,
+                        stop=True,
+                    )
+                    products = work.tile([P, ROW], F32)
+                    nc.vector.scalar_tensor_tensor(
+                        out=products[:],
+                        in0=tt[:],
+                        scalar=GAIN,
+                        in1=pb_rows[GROUP * g + c][:, s, :],
+                        op0=MULT,
+                        op1=MULT,
+                        accum_out=gain_d[:, TILES * c + s : TILES * c + s + 1],
+                    )
 
-            factor = work.tile([P, TILES], F32)
-            nc.vector.tensor_scalar_add(out=factor[:], in0=gain_d[:], scalar1=1.0)
-            out_rows = results.tile([P, TILES, ROW], F32)
-            for s in range(TILES):
+            spread = work.tile([P, GROUP * TILES, BLOCKS], F32)
+            nc.vector.tensor_tensor(
+                out=spread[:],
+                in0=gain_d[:].unsqueeze(2).to_broadcast([P, GROUP * TILES, BLOCKS]),
+                in1=in_block[:].unsqueeze(1).to_broadcast([P, GROUP * TILES, BLOCKS]),
+                op=MULT,
+            )
+            moved = psum_moved.tile([P, ROWS_HERE], F32)
+            nc.tensor.matmul(
+                out=moved[:], lhsT=spread[:].rearrange("m a b -> m (a b)"), rhs=at_offset[:], start=True, stop=True
+            )
+
+            factor = work.tile([P, ROWS_HERE], F32)
+            nc.vector.tensor_scalar_add(out=factor[:], in0=moved[:], scalar1=1.0)
+            out_rows = results.tile([P, ROWS_HERE, ROW], F32)
+            for r in range(ROWS_HERE):
                 nc.scalar.activation(
-                    out=out_rows[:, s, :], in_=feat_rows[c][:, s, :], func=COPY, scale=factor[:, s : s + 1]
+                    out=out_rows[:, r, :], in_=feat_rows[g][:, r, :], func=COPY, scale=factor[:, r : r + 1]
                 )
-            nc.sync.dma_start(out=out[c].rearrange("(s m) n -> m s n", m=P), in_=out_rows[:])
+            nc.sync.dma_start(out=out_chunks[g].rearrange("(p r) n -> p r n", r=ROWS_HERE), in_=out_rows[:])

@@ -23,7 +23,7 @@ PAIRS = ROW // 2
 QUADRANTS = 4
 GAIN = 0.3
 
-GROUP = 1
+GROUP = 2
 CHUNKS = C // GROUP
 ROWS_HERE = GROUP * ROW // P
 BLOCKS = P // ROWS_HERE
@@ -33,19 +33,22 @@ FLOPS = C * (2 * ROW * ROW * ROW + 2 * ROW * ROW + 3 * ROW * ROW)
 
 def tile_generator_pa_e_kernel(tc, Pb, Ev, W_pie_words, W_pie_scales, feat, out):
     nc = tc.nc
-    ev_chunks = Ev.rearrange("(g c) j k -> g (c j) k", c=GROUP)
     feat_chunks = feat.rearrange("(g c) i n -> g (c i) n", c=GROUP)
     out_chunks = out.rearrange("(g c) i n -> g (c i) n", c=GROUP)
 
     with ExitStack() as stack:
+        stack.enter_context(tc.manual_schedule())
         const = stack.enter_context(tc.tile_pool(name="const", bufs=1))
-        chunk_loads = stack.enter_context(tc.tile_pool(name="chunk_loads", bufs=CHUNKS))
-        pb_loads = stack.enter_context(tc.tile_pool(name="pb_loads", bufs=C))
+        loads = stack.enter_context(tc.tile_pool(name="loads", bufs=C))
+        chunks = stack.enter_context(tc.tile_pool(name="chunks", bufs=CHUNKS))
         work = stack.enter_context(tc.tile_pool(name="work", bufs=2))
-        results = stack.enter_context(tc.tile_pool(name="results", bufs=CHUNKS))
-        psum_flip = stack.enter_context(tc.psum_pool(name="psum_flip", bufs=2))
+        psum_flip = stack.enter_context(tc.psum_pool(name="psum_flip", bufs=3))
         psum_tt = stack.enter_context(tc.psum_pool(name="psum_tt", bufs=4))
-        psum_moved = stack.enter_context(tc.psum_pool(name="psum_moved", bufs=2))
+        psum_moved = stack.enter_context(tc.psum_pool(name="psum_moved", bufs=1))
+
+        w_codes = const.tile([P, C, ROW], U32, align_bytes=64)
+        w_scales = const.tile([P, C, ROW], U8, align_bytes=64)
+        nc.vector.memset(w_scales[:].rearrange("p c n -> p (c n)").bitcast(I32), 0)
 
         ident = const.tile([P, P], F32)
         make_identity(nc, ident[:])
@@ -58,95 +61,113 @@ def tile_generator_pa_e_kernel(tc, Pb, Ev, W_pie_words, W_pie_scales, feat, out)
             out=at_offset[:], in_=ident[:].rearrange("m (b r) -> m r b", r=ROWS_HERE), axis=ALONG_ROW, op=ADD
         )
 
-        w_codes = const.tile([P, C, ROW], U32, align_bytes=64)
-        w_scales = const.tile([P, C, ROW], U8, align_bytes=64)
-        nc.vector.memset(w_scales[:].rearrange("p c n -> p (c n)").bitcast(I32), 0)
-
         ev_rows, pb_rows, feat_rows = [], [], []
-        for g in range(CHUNKS):
-            ev_g = chunk_loads.tile([P, ROWS_HERE, ROW], BF16, name="ev_g", tag="ev")
-            nc.sync.dma_start(out=ev_g[:], in_=ev_chunks[g].rearrange("(p r) k -> p r k", r=ROWS_HERE))
-            ev_rows.append(ev_g)
-            if g == 0:
+        for c in range(C):
+            ev_c = loads.tile([P, TILES, ROW], BF16)
+            nc.sync.dma_start(out=ev_c[:], in_=Ev[c].rearrange("(p r) k -> p r k", r=TILES))
+            ev_rows.append(ev_c)
+            if c == 0:
                 for quad in range(QUADRANTS):
                     nc.sync.dma_start(
                         out=w_scales[32 * quad : 32 * quad + 4, :, :].bitcast(I32),
                         in_=W_pie_scales[:, 4 * quad : 4 * quad + 4, :].rearrange("c r n -> r c n").bitcast(I32),
                     )
-            for c in range(GROUP * g, GROUP * (g + 1)):
-                nc.sync.dma_start(
-                    out=w_codes[:, c, :].bitcast(I32),
-                    in_=W_pie_words[c].rearrange("p n t -> p (n t)").bitcast(I32),
-                )
-                pb_c = pb_loads.tile([P, TILES, ROW], BF16)
-                nc.sync.dma_start(out=pb_c[:], in_=Pb[c].rearrange("(s m) j -> m s j", m=P))
-                pb_rows.append(pb_c)
-            feat_g = chunk_loads.tile([P, ROWS_HERE, ROW], BF16, name="feat_g", tag="feat")
+            nc.sync.dma_start(
+                out=w_codes[:, c, :].bitcast(I32),
+                in_=W_pie_words[c].rearrange("p n t -> p (n t)").bitcast(I32),
+            )
+            pb_c = loads.tile([P, TILES, ROW], BF16)
+            nc.sync.dma_start(out=pb_c[:], in_=Pb[c].rearrange("(s m) j -> m s j", m=P))
+            pb_rows.append(pb_c)
+        for g in range(CHUNKS):
+            feat_g = chunks.tile([P, ROWS_HERE, ROW], BF16)
             nc.sync.dma_start(out=feat_g[:], in_=feat_chunks[g].rearrange("(p r) n -> p r n", r=ROWS_HERE))
             feat_rows.append(feat_g)
 
-        for g in range(CHUNKS):
-            ev_pairs = ev_rows[g][:].rearrange("p r k -> p (r k)").bitcast(F32)
-            ev_kfirst = work.tile([P, GROUP * ROW * PACK], BF16, align_bytes=64)
-            kfirst_pairs = ev_kfirst[:].bitcast(F32).rearrange("q (p h a) -> q p h a", h=ROWS_HERE // 2, a=4)
-            for h in range(ROWS_HERE // 2):
+        ev_kfirst, ev_codes, ev_scales, gain_d, spread, factors = {}, {}, {}, {}, {}, {}
+
+        def flip(c):
+            ev_pairs = ev_rows[c][:].rearrange("p r k -> p (r k)").bitcast(F32)
+            ev_kfirst[c] = work.tile([P, ROW * PACK], BF16, name="ev_kfirst", align_bytes=64)
+            kfirst_pairs = ev_kfirst[c][:].bitcast(F32).rearrange("q (p half a) -> q p half a", half=2, a=4)
+            for half in range(2):
                 flipped = psum_flip.tile([P, 4, P], F32)
                 for a in range(4):
-                    r, u = 2 * h + a // 2, a % 2
+                    r, u = 2 * half + a // 2, a % 2
                     nc.tensor.transpose(
                         flipped[:, a, :], ev_pairs[:, PAIRS * r + u : PAIRS * (r + 1) : 2], ident[:]
                     )
-                nc.scalar.copy(out=kfirst_pairs[:, :, h, :], in_=flipped[:].rearrange("q a p -> q p a"))
+                nc.scalar.copy(out=kfirst_pairs[:, :, half, :], in_=flipped[:].rearrange("q a p -> q p a"))
 
-            ev_codes = work.tile([P, GROUP, ROW], U32, align_bytes=64)
-            ev_scales = work.tile([P, GROUP, ROW], U8, align_bytes=64)
-            gain_d = work.tile([P, GROUP * TILES], F32)
-            for c in range(GROUP):
-                nc.vector.quantize_mx(
-                    out=ev_codes[:, c, :].bitcast(FP8X4),
-                    scales=ev_scales[:, c, :],
-                    in_=ev_kfirst[:, ROW * PACK * c : ROW * PACK * (c + 1)],
+        def quantise(c):
+            ev_codes[c] = work.tile([P, ROW], U32, name="ev_codes", align_bytes=64)
+            ev_scales[c] = work.tile([P, ROW], U8, name="ev_scales", align_bytes=64)
+            nc.vector.quantize_mx(out=ev_codes[c][:].bitcast(FP8X4), scales=ev_scales[c][:], in_=ev_kfirst[c][:])
+
+        def multiply(c):
+            g, first = c // GROUP, TILES * (c % GROUP)
+            if c % GROUP == 0:
+                gain_d[g] = work.tile([P, GROUP * TILES], F32, name="gain_d")
+            for s in range(TILES):
+                i_cols = slice(P * s, P * (s + 1))
+                tt = psum_tt.tile([P, ROW], F32)
+                nc.tensor.matmul_mx(
+                    out=tt[:],
+                    lhsT=w_codes[:, c, i_cols].bitcast(FP8X4),
+                    lhsT_scale=w_scales[:, c, i_cols],
+                    rhs=ev_codes[c][:].bitcast(FP8X4),
+                    rhs_scale=ev_scales[c][:],
+                    start=True,
+                    stop=True,
                 )
-                for s in range(TILES):
-                    i_cols = slice(P * s, P * (s + 1))
-                    tt = psum_tt.tile([P, ROW], F32)
-                    nc.tensor.matmul_mx(
-                        out=tt[:],
-                        lhsT=w_codes[:, GROUP * g + c, i_cols].bitcast(FP8X4),
-                        lhsT_scale=w_scales[:, GROUP * g + c, i_cols],
-                        rhs=ev_codes[:, c, :].bitcast(FP8X4),
-                        rhs_scale=ev_scales[:, c, :],
-                        start=True,
-                        stop=True,
-                    )
-                    products = work.tile([P, ROW], F32)
-                    nc.vector.scalar_tensor_tensor(
-                        out=products[:],
-                        in0=tt[:],
-                        scalar=GAIN,
-                        in1=pb_rows[GROUP * g + c][:, s, :],
-                        op0=MULT,
-                        op1=MULT,
-                        accum_out=gain_d[:, TILES * c + s : TILES * c + s + 1],
-                    )
+                products = work.tile([P, ROW], F32)
+                nc.vector.scalar_tensor_tensor(
+                    out=products[:],
+                    in0=tt[:],
+                    scalar=GAIN,
+                    in1=pb_rows[c][:, s, :],
+                    op0=MULT,
+                    op1=MULT,
+                    accum_out=gain_d[g][:, first + s : first + s + 1],
+                )
 
-            spread = work.tile([P, GROUP * TILES, BLOCKS], F32)
+        def spread_d(g):
+            spread[g] = work.tile([P, GROUP * TILES, BLOCKS], F32, name="spread")
             nc.vector.tensor_tensor(
-                out=spread[:],
-                in0=gain_d[:].unsqueeze(2).to_broadcast([P, GROUP * TILES, BLOCKS]),
+                out=spread[g][:],
+                in0=gain_d[g][:].unsqueeze(2).to_broadcast([P, GROUP * TILES, BLOCKS]),
                 in1=in_block[:].unsqueeze(1).to_broadcast([P, GROUP * TILES, BLOCKS]),
                 op=MULT,
             )
+
+        def move_d(g):
             moved = psum_moved.tile([P, ROWS_HERE], F32)
             nc.tensor.matmul(
-                out=moved[:], lhsT=spread[:].rearrange("m a b -> m (a b)"), rhs=at_offset[:], start=True, stop=True
+                out=moved[:], lhsT=spread[g][:].rearrange("m a b -> m (a b)"), rhs=at_offset[:], start=True, stop=True
             )
+            factors[g] = chunks.tile([P, ROWS_HERE], F32, name="factors")
+            nc.scalar.activation(out=factors[g][:], in_=moved[:], func=COPY, bias=1.0)
 
-            factor = work.tile([P, ROWS_HERE], F32)
-            nc.vector.tensor_scalar_add(out=factor[:], in0=moved[:], scalar1=1.0)
-            out_rows = results.tile([P, ROWS_HERE, ROW], F32)
-            for r in range(ROWS_HERE):
+        for step in range(C + 2):
+            if step < C:
+                flip(step)
+                quantise(step)
+            summed = step - 2
+            chunk_complete = summed >= 0 and summed % GROUP == GROUP - 1
+            if chunk_complete:
+                spread_d(summed // GROUP)
+            if 1 <= step <= C:
+                multiply(step - 1)
+            if chunk_complete:
+                move_d(summed // GROUP)
+
+        for g in range(CHUNKS):
+            out_rows = chunks.tile([P, ROWS_HERE, ROW], F32)
+            for r in range(0, ROWS_HERE, 2):
                 nc.scalar.activation(
-                    out=out_rows[:, r, :], in_=feat_rows[g][:, r, :], func=COPY, scale=factor[:, r : r + 1]
+                    out=out_rows[:, r, :], in_=feat_rows[g][:, r, :], func=COPY, scale=factors[g][:, r : r + 1]
+                )
+                nc.vector.tensor_scalar_mul(
+                    out=out_rows[:, r + 1, :], in0=feat_rows[g][:, r + 1, :], scalar1=factors[g][:, r + 1 : r + 2]
                 )
             nc.sync.dma_start(out=out_chunks[g].rearrange("(p r) n -> p r n", r=ROWS_HERE), in_=out_rows[:])

@@ -19,28 +19,20 @@ PACK = 4
 C = 8
 ROW = 512
 TILES = ROW // P
+BLOCKS = P // TILES
 PAIRS = ROW // 2
 QUADRANTS = 4
 GAIN = 0.3
-
-GROUP = 2
-CHUNKS = C // GROUP
-ROWS_HERE = GROUP * ROW // P
-BLOCKS = P // ROWS_HERE
 
 FLOPS = C * (2 * ROW * ROW * ROW + 2 * ROW * ROW + 3 * ROW * ROW)
 
 
 def tile_generator_pa_e_kernel(tc, Pb, Ev, W_pie_words, W_pie_scales, feat, out):
     nc = tc.nc
-    feat_chunks = feat.rearrange("(g c) i n -> g (c i) n", c=GROUP)
-    out_chunks = out.rearrange("(g c) i n -> g (c i) n", c=GROUP)
-
     with ExitStack() as stack:
         stack.enter_context(tc.manual_schedule())
         const = stack.enter_context(tc.tile_pool(name="const", bufs=1))
-        loads = stack.enter_context(tc.tile_pool(name="loads", bufs=C))
-        chunks = stack.enter_context(tc.tile_pool(name="chunks", bufs=CHUNKS))
+        resident = stack.enter_context(tc.tile_pool(name="resident", bufs=C))
         work = stack.enter_context(tc.tile_pool(name="work", bufs=2))
         psum_flip = stack.enter_context(tc.psum_pool(name="psum_flip", bufs=3))
         psum_tt = stack.enter_context(tc.psum_pool(name="psum_tt", bufs=4))
@@ -54,16 +46,16 @@ def tile_generator_pa_e_kernel(tc, Pb, Ev, W_pie_words, W_pie_scales, feat, out)
         make_identity(nc, ident[:])
         in_block = const.tile([P, BLOCKS], F32)
         nc.vector.tensor_reduce(
-            out=in_block[:], in_=ident[:].rearrange("m (b r) -> m b r", r=ROWS_HERE), axis=ALONG_ROW, op=ADD
+            out=in_block[:], in_=ident[:].rearrange("m (b r) -> m b r", r=TILES), axis=ALONG_ROW, op=ADD
         )
-        at_offset = const.tile([P, ROWS_HERE], F32)
+        at_offset = const.tile([P, TILES], F32)
         nc.vector.tensor_reduce(
-            out=at_offset[:], in_=ident[:].rearrange("m (b r) -> m r b", r=ROWS_HERE), axis=ALONG_ROW, op=ADD
+            out=at_offset[:], in_=ident[:].rearrange("m (b r) -> m r b", r=TILES), axis=ALONG_ROW, op=ADD
         )
 
         ev_rows, pb_rows, feat_rows = [], [], []
         for c in range(C):
-            ev_c = loads.tile([P, TILES, ROW], BF16)
+            ev_c = resident.tile([P, TILES, ROW], BF16)
             nc.sync.dma_start(out=ev_c[:], in_=Ev[c].rearrange("(p r) k -> p r k", r=TILES))
             ev_rows.append(ev_c)
             if c == 0:
@@ -76,13 +68,12 @@ def tile_generator_pa_e_kernel(tc, Pb, Ev, W_pie_words, W_pie_scales, feat, out)
                 out=w_codes[:, c, :].bitcast(I32),
                 in_=W_pie_words[c].rearrange("p n t -> p (n t)").bitcast(I32),
             )
-            pb_c = loads.tile([P, TILES, ROW], BF16)
+            pb_c = resident.tile([P, TILES, ROW], BF16)
             nc.sync.dma_start(out=pb_c[:], in_=Pb[c].rearrange("(s m) j -> m s j", m=P))
             pb_rows.append(pb_c)
-        for g in range(CHUNKS):
-            feat_g = chunks.tile([P, ROWS_HERE, ROW], BF16)
-            nc.sync.dma_start(out=feat_g[:], in_=feat_chunks[g].rearrange("(p r) n -> p r n", r=ROWS_HERE))
-            feat_rows.append(feat_g)
+            feat_c = resident.tile([P, TILES, ROW], BF16)
+            nc.sync.dma_start(out=feat_c[:], in_=feat[c].rearrange("(p r) n -> p r n", r=TILES))
+            feat_rows.append(feat_c)
 
         ev_kfirst, ev_codes, ev_scales, gain_d, spread, factors = {}, {}, {}, {}, {}, {}
 
@@ -105,9 +96,7 @@ def tile_generator_pa_e_kernel(tc, Pb, Ev, W_pie_words, W_pie_scales, feat, out)
             nc.vector.quantize_mx(out=ev_codes[c][:].bitcast(FP8X4), scales=ev_scales[c][:], in_=ev_kfirst[c][:])
 
         def multiply(c):
-            g, first = c // GROUP, TILES * (c % GROUP)
-            if c % GROUP == 0:
-                gain_d[g] = work.tile([P, GROUP * TILES], F32, name="gain_d")
+            gain_d[c] = work.tile([P, TILES], F32, name="gain_d")
             for s in range(TILES):
                 i_cols = slice(P * s, P * (s + 1))
                 tt = psum_tt.tile([P, ROW], F32)
@@ -128,46 +117,46 @@ def tile_generator_pa_e_kernel(tc, Pb, Ev, W_pie_words, W_pie_scales, feat, out)
                     in1=pb_rows[c][:, s, :],
                     op0=MULT,
                     op1=MULT,
-                    accum_out=gain_d[g][:, first + s : first + s + 1],
+                    accum_out=gain_d[c][:, s : s + 1],
                 )
 
-        def spread_d(g):
-            spread[g] = work.tile([P, GROUP * TILES, BLOCKS], F32, name="spread")
+        def spread_d(c):
+            spread[c] = work.tile([P, TILES, BLOCKS], F32, name="spread")
             nc.vector.tensor_tensor(
-                out=spread[g][:],
-                in0=gain_d[g][:].unsqueeze(2).to_broadcast([P, GROUP * TILES, BLOCKS]),
-                in1=in_block[:].unsqueeze(1).to_broadcast([P, GROUP * TILES, BLOCKS]),
+                out=spread[c][:],
+                in0=gain_d[c][:].unsqueeze(2).to_broadcast([P, TILES, BLOCKS]),
+                in1=in_block[:].unsqueeze(1).to_broadcast([P, TILES, BLOCKS]),
                 op=MULT,
             )
 
-        def move_d(g):
-            moved = psum_moved.tile([P, ROWS_HERE], F32)
+        def move_d(c):
+            moved = psum_moved.tile([P, TILES], F32)
             nc.tensor.matmul(
-                out=moved[:], lhsT=spread[g][:].rearrange("m a b -> m (a b)"), rhs=at_offset[:], start=True, stop=True
+                out=moved[:], lhsT=spread[c][:].rearrange("m s b -> m (s b)"), rhs=at_offset[:], start=True, stop=True
             )
-            factors[g] = chunks.tile([P, ROWS_HERE], F32, name="factors")
-            nc.scalar.activation(out=factors[g][:], in_=moved[:], func=COPY, bias=1.0)
+            factors[c] = work.tile([P, TILES], F32, name="factors")
+            nc.scalar.activation(out=factors[c][:], in_=moved[:], func=COPY, bias=1.0)
 
-        for step in range(C + 2):
-            if step < C:
+        def scale_and_store(c):
+            out_rows = resident.tile([P, TILES, ROW], F32)
+            for r in range(TILES):
+                nc.scalar.activation(
+                    out=out_rows[:, r, :], in_=feat_rows[c][:, r, :], func=COPY, scale=factors[c][:, r : r + 1]
+                )
+            nc.sync.dma_start(out=out[c].rearrange("(p r) n -> p r n", r=TILES), in_=out_rows[:])
+
+        def in_range(c):
+            return 0 <= c < C
+
+        for step in range(C + 3):
+            if in_range(step):
                 flip(step)
                 quantise(step)
-            summed = step - 2
-            chunk_complete = summed >= 0 and summed % GROUP == GROUP - 1
-            if chunk_complete:
-                spread_d(summed // GROUP)
-            if 1 <= step <= C:
+            if in_range(step - 2):
+                spread_d(step - 2)
+            if in_range(step - 3):
+                scale_and_store(step - 3)
+            if in_range(step - 1):
                 multiply(step - 1)
-            if chunk_complete:
-                move_d(summed // GROUP)
-
-        for g in range(CHUNKS):
-            out_rows = chunks.tile([P, ROWS_HERE, ROW], F32)
-            for r in range(0, ROWS_HERE, 2):
-                nc.scalar.activation(
-                    out=out_rows[:, r, :], in_=feat_rows[g][:, r, :], func=COPY, scale=factors[g][:, r : r + 1]
-                )
-                nc.vector.tensor_scalar_mul(
-                    out=out_rows[:, r + 1, :], in0=feat_rows[g][:, r + 1, :], scalar1=factors[g][:, r + 1 : r + 2]
-                )
-            nc.sync.dma_start(out=out_chunks[g].rearrange("(p r) n -> p r n", r=ROWS_HERE), in_=out_rows[:])
+            if in_range(step - 2):
+                move_d(step - 2)

@@ -23,6 +23,7 @@ BLOCKS = P // TILES
 PAIRS = ROW // 2
 QUADRANTS = 4
 GAIN = 0.3
+GROUP = 2
 
 FLOPS = C * (2 * ROW * ROW * ROW + 2 * ROW * ROW + 3 * ROW * ROW)
 
@@ -32,7 +33,7 @@ def tile_generator_pa_e_kernel(tc, Pb, Ev, W_pie_words, W_pie_scales, feat, out)
     with ExitStack() as stack:
         stack.enter_context(tc.manual_schedule())
         const = stack.enter_context(tc.tile_pool(name="const", bufs=1))
-        resident = stack.enter_context(tc.tile_pool(name="resident", bufs=C))
+        resident = stack.enter_context(tc.tile_pool(name="resident", bufs=C // GROUP))
         work = stack.enter_context(tc.tile_pool(name="work", bufs=2))
         psum_flip = stack.enter_context(tc.psum_pool(name="psum_flip", bufs=3))
         psum_tt = stack.enter_context(tc.psum_pool(name="psum_tt", bufs=4))
@@ -54,31 +55,33 @@ def tile_generator_pa_e_kernel(tc, Pb, Ev, W_pie_words, W_pie_scales, feat, out)
         )
 
         ev_rows, pb_rows, feat_rows = [], [], []
-        for c in range(C):
-            ev_c = resident.tile([P, TILES, ROW], BF16)
-            nc.sync.dma_start(out=ev_c[:], in_=Ev[c].rearrange("(p r) k -> p r k", r=TILES))
-            ev_rows.append(ev_c)
-            if c == 0:
+        for g in range(C // GROUP):
+            cs = slice(GROUP * g, GROUP * (g + 1))
+            ev_g = resident.tile([P, GROUP, TILES, ROW], BF16)
+            nc.sync.dma_start(out=ev_g[:], in_=Ev[cs].rearrange("c (p r) k -> p c r k", r=TILES))
+            if g == 0:
                 for quad in range(QUADRANTS):
                     nc.sync.dma_start(
                         out=w_scales[32 * quad : 32 * quad + 4, :, :].bitcast(I32),
                         in_=W_pie_scales[:, 4 * quad : 4 * quad + 4, :].rearrange("c r n -> r c n").bitcast(I32),
                     )
             nc.sync.dma_start(
-                out=w_codes[:, c, :].bitcast(I32),
-                in_=W_pie_words[c].rearrange("p n t -> p (n t)").bitcast(I32),
+                out=w_codes[:, cs, :].bitcast(I32),
+                in_=W_pie_words[cs].rearrange("c p n t -> p c (n t)").bitcast(I32),
             )
-            pb_c = resident.tile([P, TILES, ROW], BF16)
-            nc.sync.dma_start(out=pb_c[:], in_=Pb[c].rearrange("(s m) j -> m s j", m=P))
-            pb_rows.append(pb_c)
-            feat_c = resident.tile([P, TILES, ROW], BF16)
-            nc.sync.dma_start(out=feat_c[:], in_=feat[c].rearrange("(p r) n -> p r n", r=TILES))
-            feat_rows.append(feat_c)
+            pb_g = resident.tile([P, GROUP, TILES, ROW], BF16)
+            nc.sync.dma_start(out=pb_g[:], in_=Pb[cs].rearrange("c (s m) j -> m c s j", m=P))
+            feat_g = resident.tile([P, GROUP, TILES, ROW], BF16)
+            nc.sync.dma_start(out=feat_g[:], in_=feat[cs].rearrange("c (p r) n -> p c r n", r=TILES))
+            for cc in range(GROUP):
+                ev_rows.append(ev_g[:, cc])
+                pb_rows.append(pb_g[:, cc])
+                feat_rows.append(feat_g[:, cc])
 
-        ev_kfirst, ev_codes, ev_scales, gain_d, spread, factors = {}, {}, {}, {}, {}, {}
+        ev_kfirst, ev_codes, ev_scales, gain_d, spread, factors, out_groups = {}, {}, {}, {}, {}, {}, {}
 
         def flip(c):
-            ev_pairs = ev_rows[c][:].rearrange("p r k -> p (r k)").bitcast(F32)
+            ev_pairs = ev_rows[c].rearrange("p r k -> p (r k)").bitcast(F32)
             ev_kfirst[c] = work.tile([P, ROW * PACK], BF16, name="ev_kfirst", align_bytes=64)
             kfirst_pairs = ev_kfirst[c][:].bitcast(F32).rearrange("q (p half a) -> q p half a", half=2, a=4)
             for half in range(2):
@@ -138,12 +141,17 @@ def tile_generator_pa_e_kernel(tc, Pb, Ev, W_pie_words, W_pie_scales, feat, out)
             nc.scalar.activation(out=factors[c][:], in_=moved[:], func=COPY, bias=1.0)
 
         def scale_and_store(c):
-            out_rows = resident.tile([P, TILES, ROW], F32)
+            g, cc = c // GROUP, c % GROUP
+            if cc == 0:
+                out_groups[g] = resident.tile([P, GROUP, TILES, ROW], F32, name="out_g")
             for r in range(TILES):
                 nc.scalar.activation(
-                    out=out_rows[:, r, :], in_=feat_rows[c][:, r, :], func=COPY, scale=factors[c][:, r : r + 1]
+                    out=out_groups[g][:, cc, r, :], in_=feat_rows[c][:, r, :], func=COPY, scale=factors[c][:, r : r + 1]
                 )
-            nc.sync.dma_start(out=out[c].rearrange("(p r) n -> p r n", r=TILES), in_=out_rows[:])
+            if cc == GROUP - 1:
+                nc.sync.dma_start(
+                    out=out[GROUP * g : GROUP * (g + 1)].rearrange("c (p r) n -> p c r n", r=TILES), in_=out_groups[g][:]
+                )
 
         def in_range(c):
             return 0 <= c < C

@@ -24,6 +24,7 @@ PAIRS = ROW // 2
 QUADRANTS = 4
 GAIN = 0.3
 GROUP = 2
+PLANES = 4
 
 FLOPS = C * (2 * ROW * ROW * ROW + 2 * ROW * ROW + 3 * ROW * ROW)
 
@@ -40,8 +41,8 @@ def tile_generator_pa_e_kernel(tc, Pb, Ev, W_pie_words, W_pie_scales, feat, out)
         psum_moved = stack.enter_context(tc.psum_pool(name="psum_moved", bufs=1))
 
         w_codes = const.tile([P, C, ROW], U32, align_bytes=64)
-        w_scales = const.tile([P, C, ROW], U8, align_bytes=64)
-        nc.vector.memset(w_scales[:].rearrange("p c n -> p (c n)").bitcast(I32), 0)
+        w_scales = const.tile([P, C // PLANES, ROW], U8, align_bytes=64)
+        nc.vector.memset(w_scales[:].rearrange("p a n -> p (a n)").bitcast(I32), 0)
 
         ident = const.tile([P, P], F32)
         make_identity(nc, ident[:])
@@ -60,11 +61,12 @@ def tile_generator_pa_e_kernel(tc, Pb, Ev, W_pie_words, W_pie_scales, feat, out)
             ev_g = resident.tile([P, GROUP, TILES, ROW], BF16)
             nc.sync.dma_start(out=ev_g[:], in_=Ev[cs].rearrange("c (p r) k -> p c r k", r=TILES))
             if g == 0:
-                for quad in range(QUADRANTS):
-                    nc.sync.dma_start(
-                        out=w_scales[32 * quad : 32 * quad + 4, :, :].bitcast(I32),
-                        in_=W_pie_scales[:, 4 * quad : 4 * quad + 4, :].rearrange("c r n -> r c n").bitcast(I32),
-                    )
+                for a in range(C // PLANES):
+                    for quad in range(QUADRANTS):
+                        nc.sync.dma_start(
+                            out=w_scales[32 * quad : 32 * quad + 16, a, :].bitcast(I32),
+                            in_=W_pie_scales[PLANES * a : PLANES * (a + 1), 4 * quad : 4 * quad + 4, :].bitcast(I32),
+                        )
             nc.sync.dma_start(
                 out=w_codes[:, cs, :].bitcast(I32),
                 in_=W_pie_words[cs].rearrange("c p n t -> p c (n t)").bitcast(I32),
@@ -106,7 +108,7 @@ def tile_generator_pa_e_kernel(tc, Pb, Ev, W_pie_words, W_pie_scales, feat, out)
                 nc.tensor.matmul_mx(
                     out=tt[:],
                     lhsT=w_codes[:, c, i_cols].bitcast(FP8X4),
-                    lhsT_scale=w_scales[:, c, i_cols],
+                    lhsT_scale=w_scales[4 * (c % PLANES) : P, c // PLANES, i_cols],
                     rhs=ev_codes[c][:].bitcast(FP8X4),
                     rhs_scale=ev_scales[c][:],
                     start=True,

@@ -9,17 +9,14 @@ I32 = mybir.dt.int32
 U32 = mybir.dt.uint32
 U8 = mybir.dt.uint8
 FP8X4 = mybir.dt.float8_e4m3fn_x4
-ADD = mybir.AluOpType.add
 MULT = mybir.AluOpType.mult
 COPY = mybir.ActivationFunctionType.Copy
-ALONG_ROW = mybir.AxisListType.X
 
 P = 128
 PACK = 4
 C = 8
 ROW = 512
 TILES = ROW // P
-BLOCKS = P // TILES
 PAIRS = ROW // 2
 QUADRANTS = 4
 GAIN = 0.3
@@ -38,41 +35,33 @@ def tile_generator_pa_e_kernel(tc, Pb, Ev, W_pie_words, W_pie_scales, feat, out)
         work = stack.enter_context(tc.tile_pool(name="work", bufs=2))
         psum_flip = stack.enter_context(tc.psum_pool(name="psum_flip", bufs=3))
         psum_tt = stack.enter_context(tc.psum_pool(name="psum_tt", bufs=4))
-        psum_moved = stack.enter_context(tc.psum_pool(name="psum_moved", bufs=1))
 
+        w_arrived = const.tile([P, C, ROW], U32)
         w_codes = const.tile([P, C, ROW], U32, align_bytes=64)
+        s_arrived = const.tile([P, C // PLANES, ROW], U8)
+        nc.vector.memset(s_arrived[:].rearrange("p a n -> p (a n)").bitcast(I32), 0)
         w_scales = const.tile([P, C // PLANES, ROW], U8, align_bytes=64)
-        nc.vector.memset(w_scales[:].rearrange("p a n -> p (a n)").bitcast(I32), 0)
 
         ident = const.tile([P, P], F32)
         make_identity(nc, ident[:])
-        in_block = const.tile([P, BLOCKS], F32)
-        nc.vector.tensor_reduce(
-            out=in_block[:], in_=ident[:].rearrange("m (b r) -> m b r", r=TILES), axis=ALONG_ROW, op=ADD
-        )
-        at_offset = const.tile([P, TILES], F32)
-        nc.vector.tensor_reduce(
-            out=at_offset[:], in_=ident[:].rearrange("m (b r) -> m r b", r=TILES), axis=ALONG_ROW, op=ADD
-        )
-
         ev_rows, pb_rows, feat_rows = [], [], []
         for g in range(C // GROUP):
             cs = slice(GROUP * g, GROUP * (g + 1))
             ev_g = resident.tile([P, GROUP, TILES, ROW], BF16)
             nc.sync.dma_start(out=ev_g[:], in_=Ev[cs].rearrange("c (p r) k -> p c r k", r=TILES))
+            nc.sync.dma_start(
+                out=w_arrived[:, cs, :].bitcast(I32),
+                in_=W_pie_words[cs].rearrange("c p n t -> p c (n t)").bitcast(I32),
+            )
             if g == 0:
                 for a in range(C // PLANES):
                     for quad in range(QUADRANTS):
                         nc.sync.dma_start(
-                            out=w_scales[32 * quad : 32 * quad + 16, a, :].bitcast(I32),
+                            out=s_arrived[32 * quad : 32 * quad + 16, a, :].bitcast(I32),
                             in_=W_pie_scales[PLANES * a : PLANES * (a + 1), 4 * quad : 4 * quad + 4, :].bitcast(I32),
                         )
-            nc.sync.dma_start(
-                out=w_codes[:, cs, :].bitcast(I32),
-                in_=W_pie_words[cs].rearrange("c p n t -> p c (n t)").bitcast(I32),
-            )
             pb_g = resident.tile([P, GROUP, TILES, ROW], BF16)
-            nc.sync.dma_start(out=pb_g[:], in_=Pb[cs].rearrange("c (s m) j -> m c s j", m=P))
+            nc.sync.dma_start(out=pb_g[:], in_=Pb[cs].rearrange("c (m r) j -> m c r j", r=TILES))
             feat_g = resident.tile([P, GROUP, TILES, ROW], BF16)
             nc.sync.dma_start(out=feat_g[:], in_=feat[cs].rearrange("c (p r) n -> p c r n", r=TILES))
             for cc in range(GROUP):
@@ -80,7 +69,7 @@ def tile_generator_pa_e_kernel(tc, Pb, Ev, W_pie_words, W_pie_scales, feat, out)
                 pb_rows.append(pb_g[:, cc])
                 feat_rows.append(feat_g[:, cc])
 
-        ev_kfirst, ev_codes, ev_scales, gain_d, spread, factors, out_groups = {}, {}, {}, {}, {}, {}, {}
+        ev_kfirst, ev_codes, ev_scales, gain_d, factors, out_groups = {}, {}, {}, {}, {}, {}
 
         def flip(c):
             ev_pairs = ev_rows[c].rearrange("p r k -> p (r k)").bitcast(F32)
@@ -100,10 +89,23 @@ def tile_generator_pa_e_kernel(tc, Pb, Ev, W_pie_words, W_pie_scales, feat, out)
             ev_scales[c] = work.tile([P, ROW], U8, name="ev_scales", align_bytes=64)
             nc.vector.quantize_mx(out=ev_codes[c][:].bitcast(FP8X4), scales=ev_scales[c][:], in_=ev_kfirst[c][:])
 
+        def reorder_scales():
+            for a in range(C // PLANES):
+                nc.vector.tensor_copy(
+                    out=w_scales[:, a, :].rearrange("p (r m) -> p m r", r=TILES),
+                    in_=s_arrived[:, a, :].rearrange("p (m r) -> p m r", r=TILES),
+                )
+
+        def reorder(c):
+            nc.vector.tensor_copy(
+                out=w_codes[:, c, :].bitcast(I32).rearrange("p (r m) -> p r m", r=TILES),
+                in_=w_arrived[:, c, :].bitcast(I32).rearrange("p (m r) -> p r m", r=TILES),
+            )
+
         def multiply(c):
             gain_d[c] = work.tile([P, TILES], F32, name="gain_d")
-            for s in range(TILES):
-                i_cols = slice(P * s, P * (s + 1))
+            for r in range(TILES):
+                i_cols = slice(P * r, P * (r + 1))
                 tt = psum_tt.tile([P, ROW], F32)
                 nc.tensor.matmul_mx(
                     out=tt[:],
@@ -119,28 +121,13 @@ def tile_generator_pa_e_kernel(tc, Pb, Ev, W_pie_words, W_pie_scales, feat, out)
                     out=products[:],
                     in0=tt[:],
                     scalar=GAIN,
-                    in1=pb_rows[c][:, s, :],
+                    in1=pb_rows[c][:, r, :],
                     op0=MULT,
                     op1=MULT,
-                    accum_out=gain_d[c][:, s : s + 1],
+                    accum_out=gain_d[c][:, r : r + 1],
                 )
-
-        def spread_d(c):
-            spread[c] = work.tile([P, TILES, BLOCKS], F32, name="spread")
-            nc.vector.tensor_tensor(
-                out=spread[c][:],
-                in0=gain_d[c][:].unsqueeze(2).to_broadcast([P, TILES, BLOCKS]),
-                in1=in_block[:].unsqueeze(1).to_broadcast([P, TILES, BLOCKS]),
-                op=MULT,
-            )
-
-        def move_d(c):
-            moved = psum_moved.tile([P, TILES], F32)
-            nc.tensor.matmul(
-                out=moved[:], lhsT=spread[c][:].rearrange("m s b -> m (s b)"), rhs=at_offset[:], start=True, stop=True
-            )
             factors[c] = work.tile([P, TILES], F32, name="factors")
-            nc.scalar.activation(out=factors[c][:], in_=moved[:], func=COPY, bias=1.0)
+            nc.scalar.activation(out=factors[c][:], in_=gain_d[c][:], func=COPY, bias=1.0)
 
         def scale_and_store(c):
             g, cc = c // GROUP, c % GROUP
@@ -158,15 +145,13 @@ def tile_generator_pa_e_kernel(tc, Pb, Ev, W_pie_words, W_pie_scales, feat, out)
         def in_range(c):
             return 0 <= c < C
 
-        for step in range(C + 3):
+        reorder_scales()
+        for step in range(C + 2):
             if in_range(step):
                 flip(step)
                 quantise(step)
+                reorder(step)
             if in_range(step - 2):
-                spread_d(step - 2)
-            if in_range(step - 3):
-                scale_and_store(step - 3)
+                scale_and_store(step - 2)
             if in_range(step - 1):
                 multiply(step - 1)
-            if in_range(step - 2):
-                move_d(step - 2)

@@ -9,6 +9,7 @@ I32 = mybir.dt.int32
 U32 = mybir.dt.uint32
 U8 = mybir.dt.uint8
 FP8X4 = mybir.dt.float8_e4m3fn_x4
+ADD = mybir.AluOpType.add
 MULT = mybir.AluOpType.mult
 COPY = mybir.ActivationFunctionType.Copy
 
@@ -33,7 +34,7 @@ def tile_generator_pa_e_kernel(tc, Pb, Ev, W_pie_words, W_pie_scales, feat, out)
         const = stack.enter_context(tc.tile_pool(name="const", bufs=1))
         resident = stack.enter_context(tc.tile_pool(name="resident", bufs=C // GROUP))
         work = stack.enter_context(tc.tile_pool(name="work", bufs=2))
-        psum_flip = stack.enter_context(tc.psum_pool(name="psum_flip", bufs=3))
+        psum_flip = stack.enter_context(tc.psum_pool(name="psum_flip", bufs=4))
         psum_tt = stack.enter_context(tc.psum_pool(name="psum_tt", bufs=4))
 
         w_arrived = const.tile([P, C, ROW], U32)
@@ -53,13 +54,13 @@ def tile_generator_pa_e_kernel(tc, Pb, Ev, W_pie_words, W_pie_scales, feat, out)
                 out=w_arrived[:, cs, :].bitcast(I32),
                 in_=W_pie_words[cs].rearrange("c p n t -> p c (n t)").bitcast(I32),
             )
-            if g == 0:
-                for a in range(C // PLANES):
-                    for quad in range(QUADRANTS):
-                        nc.sync.dma_start(
-                            out=s_arrived[32 * quad : 32 * quad + 16, a, :].bitcast(I32),
-                            in_=W_pie_scales[PLANES * a : PLANES * (a + 1), 4 * quad : 4 * quad + 4, :].bitcast(I32),
-                        )
+            if (GROUP * g) % PLANES == 0:
+                a = GROUP * g // PLANES
+                for quad in range(QUADRANTS):
+                    nc.sync.dma_start(
+                        out=s_arrived[32 * quad : 32 * quad + 16, a, :].bitcast(I32),
+                        in_=W_pie_scales[PLANES * a : PLANES * (a + 1), 4 * quad : 4 * quad + 4, :].bitcast(I32),
+                    )
             pb_g = resident.tile([P, GROUP, TILES, ROW], BF16)
             nc.sync.dma_start(out=pb_g[:], in_=Pb[cs].rearrange("c (m r) j -> m c r j", r=TILES))
             feat_g = resident.tile([P, GROUP, TILES, ROW], BF16)
@@ -69,32 +70,34 @@ def tile_generator_pa_e_kernel(tc, Pb, Ev, W_pie_words, W_pie_scales, feat, out)
                 pb_rows.append(pb_g[:, cc])
                 feat_rows.append(feat_g[:, cc])
 
-        ev_kfirst, ev_codes, ev_scales, gain_d, factors, out_groups = {}, {}, {}, {}, {}, {}
+        flipped, ev_kfirst, ev_codes, ev_scales, tt, gain_d, factors, out_groups = {}, {}, {}, {}, {}, {}, {}, {}
 
-        def flip(c):
+        def transposes(c):
             ev_pairs = ev_rows[c].rearrange("p r k -> p (r k)").bitcast(F32)
-            ev_kfirst[c] = work.tile([P, ROW * PACK], BF16, name="ev_kfirst", align_bytes=64)
-            kfirst_pairs = ev_kfirst[c][:].bitcast(F32).rearrange("q (p half a) -> q p half a", half=2, a=4)
             for half in range(2):
-                flipped = psum_flip.tile([P, 4, P], F32)
+                flipped[c, half] = psum_flip.tile([P, 4, P], F32, name="flipped")
                 for a in range(4):
                     r, u = 2 * half + a // 2, a % 2
                     nc.tensor.transpose(
-                        flipped[:, a, :], ev_pairs[:, PAIRS * r + u : PAIRS * (r + 1) : 2], ident[:]
+                        flipped[c, half][:, a, :], ev_pairs[:, PAIRS * r + u : PAIRS * (r + 1) : 2], ident[:]
                     )
-                nc.scalar.copy(out=kfirst_pairs[:, :, half, :], in_=flipped[:].rearrange("q a p -> q p a"))
+
+        def copies(c):
+            ev_kfirst[c] = work.tile([P, ROW * PACK], BF16, name="ev_kfirst", align_bytes=64)
+            kfirst_pairs = ev_kfirst[c][:].bitcast(F32).rearrange("q (p half a) -> q p half a", half=2, a=4)
+            for half in range(2):
+                nc.scalar.copy(out=kfirst_pairs[:, :, half, :], in_=flipped[c, half][:].rearrange("q a p -> q p a"))
 
         def quantise(c):
             ev_codes[c] = work.tile([P, ROW], U32, name="ev_codes", align_bytes=64)
             ev_scales[c] = work.tile([P, ROW], U8, name="ev_scales", align_bytes=64)
             nc.vector.quantize_mx(out=ev_codes[c][:].bitcast(FP8X4), scales=ev_scales[c][:], in_=ev_kfirst[c][:])
 
-        def reorder_scales():
-            for a in range(C // PLANES):
-                nc.vector.tensor_copy(
-                    out=w_scales[:, a, :].rearrange("p (r m) -> p m r", r=TILES),
-                    in_=s_arrived[:, a, :].rearrange("p (m r) -> p m r", r=TILES),
-                )
+        def reorder_scales(a):
+            nc.vector.tensor_copy(
+                out=w_scales[:, a, :].rearrange("p (r m) -> p m r", r=TILES),
+                in_=s_arrived[:, a, :].rearrange("p (m r) -> p m r", r=TILES),
+            )
 
         def reorder(c):
             nc.vector.tensor_copy(
@@ -102,13 +105,12 @@ def tile_generator_pa_e_kernel(tc, Pb, Ev, W_pie_words, W_pie_scales, feat, out)
                 in_=w_arrived[:, c, :].bitcast(I32).rearrange("p (m r) -> p r m", r=TILES),
             )
 
-        def multiply(c):
-            gain_d[c] = work.tile([P, TILES], F32, name="gain_d")
+        def passes(c):
             for r in range(TILES):
                 i_cols = slice(P * r, P * (r + 1))
-                tt = psum_tt.tile([P, ROW], F32)
+                tt[c, r] = psum_tt.tile([P, ROW], F32, name="tt")
                 nc.tensor.matmul_mx(
-                    out=tt[:],
+                    out=tt[c, r][:],
                     lhsT=w_codes[:, c, i_cols].bitcast(FP8X4),
                     lhsT_scale=w_scales[4 * (c % PLANES) : P, c // PLANES, i_cols],
                     rhs=ev_codes[c][:].bitcast(FP8X4),
@@ -116,18 +118,24 @@ def tile_generator_pa_e_kernel(tc, Pb, Ev, W_pie_words, W_pie_scales, feat, out)
                     start=True,
                     stop=True,
                 )
-                products = work.tile([P, ROW], F32)
-                nc.vector.scalar_tensor_tensor(
-                    out=products[:],
-                    in0=tt[:],
-                    scalar=GAIN,
-                    in1=pb_rows[c][:, r, :],
-                    op0=MULT,
-                    op1=MULT,
-                    accum_out=gain_d[c][:, r : r + 1],
-                )
+
+        def products(c, r):
+            if r == 0:
+                gain_d[c] = work.tile([P, TILES], F32, name="gain_d")
+            scratch = work.tile([P, ROW], F32, name="scratch")
+            nc.vector.scalar_tensor_tensor(
+                out=scratch[:],
+                in0=tt[c, r][:],
+                scalar=GAIN,
+                in1=pb_rows[c][:, r, :],
+                op0=MULT,
+                op1=MULT,
+                accum_out=gain_d[c][:, r : r + 1],
+            )
+
+        def make_factors(c):
             factors[c] = work.tile([P, TILES], F32, name="factors")
-            nc.scalar.activation(out=factors[c][:], in_=gain_d[c][:], func=COPY, bias=1.0)
+            nc.vector.tensor_scalar(out=factors[c][:], in0=gain_d[c][:], scalar1=1.0, scalar2=None, op0=ADD)
 
         def scale_and_store(c):
             g, cc = c // GROUP, c % GROUP
@@ -145,13 +153,30 @@ def tile_generator_pa_e_kernel(tc, Pb, Ev, W_pie_words, W_pie_scales, feat, out)
         def in_range(c):
             return 0 <= c < C
 
-        reorder_scales()
-        for step in range(C + 2):
-            if in_range(step):
-                flip(step)
-                quantise(step)
-                reorder(step)
-            if in_range(step - 2):
-                scale_and_store(step - 2)
-            if in_range(step - 1):
-                multiply(step - 1)
+        for c in range(2):
+            transposes(c)
+            copies(c)
+        reorder_scales(0)
+        reorder(0)
+        quantise(0)
+        for c in range(C + 1):
+            if in_range(c):
+                passes(c)
+            if in_range(c + 2):
+                transposes(c + 2)
+            if in_range(c):
+                products(c, 0)
+                products(c, 1)
+            if in_range(c + 1):
+                if (c + 1) % PLANES == 0:
+                    reorder_scales((c + 1) // PLANES)
+                reorder(c + 1)
+                quantise(c + 1)
+            if in_range(c):
+                products(c, 2)
+                products(c, 3)
+                make_factors(c)
+            if in_range(c - 1):
+                scale_and_store(c - 1)
+            if in_range(c + 2):
+                copies(c + 2)

@@ -11,6 +11,7 @@ U8 = mybir.dt.uint8
 FP8X4 = mybir.dt.float8_e4m3fn_x4
 ADD = mybir.AluOpType.add
 MULT = mybir.AluOpType.mult
+ALONG_ROW = mybir.AxisListType.X
 COPY = mybir.ActivationFunctionType.Copy
 
 P = 128
@@ -22,6 +23,8 @@ PAIRS = ROW // 2
 QUADRANTS = 4
 GAIN = 0.3
 GROUP = 2
+LONG = GROUP * TILES
+SPAN = P // GROUP
 PLANES = 4
 
 FLOPS = C * (2 * ROW * ROW * ROW + 2 * ROW * ROW + 3 * ROW * ROW)
@@ -34,8 +37,9 @@ def tile_generator_pa_e_kernel(tc, Pb, Ev, W_pie_words, W_pie_scales, feat, out)
         const = stack.enter_context(tc.tile_pool(name="const", bufs=1))
         resident = stack.enter_context(tc.tile_pool(name="resident", bufs=C // GROUP))
         work = stack.enter_context(tc.tile_pool(name="work", bufs=2))
-        psum_flip = stack.enter_context(tc.psum_pool(name="psum_flip", bufs=4))
+        psum_flip = stack.enter_context(tc.psum_pool(name="psum_flip", bufs=3))
         psum_tt = stack.enter_context(tc.psum_pool(name="psum_tt", bufs=4))
+        psum_moved = stack.enter_context(tc.psum_pool(name="psum_moved", bufs=1))
 
         w_arrived = const.tile([P, C, ROW], U32)
         w_codes = const.tile([P, C, ROW], U32, align_bytes=64)
@@ -45,6 +49,18 @@ def tile_generator_pa_e_kernel(tc, Pb, Ev, W_pie_words, W_pie_scales, feat, out)
 
         ident = const.tile([P, P], F32)
         make_identity(nc, ident[:])
+        in_span = const.tile([P, SPAN], F32)
+        nc.vector.tensor_reduce(
+            out=in_span[:], in_=ident[:].rearrange("m (b e) -> m b e", e=GROUP), axis=ALONG_ROW, op=ADD
+        )
+        at_part = const.tile([P, GROUP], F32)
+        nc.vector.tensor_reduce(
+            out=at_part[:], in_=ident[:].rearrange("m (b e) -> m e b", e=GROUP), axis=ALONG_ROW, op=ADD
+        )
+        carry = const.tile([P, GROUP, P], F32)
+        nc.vector.memset(carry[:], 0.0)
+        for cc in range(GROUP):
+            nc.vector.tensor_copy(out=carry[:, cc, SPAN * cc : SPAN * (cc + 1)], in_=in_span[:])
         ev_rows, pb_rows, feat_rows = [], [], []
         for g in range(C // GROUP):
             cs = slice(GROUP * g, GROUP * (g + 1))
@@ -63,14 +79,16 @@ def tile_generator_pa_e_kernel(tc, Pb, Ev, W_pie_words, W_pie_scales, feat, out)
                     )
             pb_g = resident.tile([P, GROUP, TILES, ROW], BF16)
             nc.sync.dma_start(out=pb_g[:], in_=Pb[cs].rearrange("c (m r) j -> m c r j", r=TILES))
-            feat_g = resident.tile([P, GROUP, TILES, ROW], BF16)
-            nc.sync.dma_start(out=feat_g[:], in_=feat[cs].rearrange("c (p r) n -> p c r n", r=TILES))
+            feat_g = resident.tile([P, LONG, ROW], BF16)
+            nc.sync.dma_start(
+                out=feat_g[:], in_=feat[cs].rearrange("c i n -> (c i) n").rearrange("(p l) n -> p l n", l=LONG)
+            )
+            feat_rows.append(feat_g)
             for cc in range(GROUP):
                 ev_rows.append(ev_g[:, cc])
                 pb_rows.append(pb_g[:, cc])
-                feat_rows.append(feat_g[:, cc])
 
-        flipped, ev_kfirst, ev_codes, ev_scales, tt, gain_d, factors, out_groups = {}, {}, {}, {}, {}, {}, {}, {}
+        flipped, ev_kfirst, ev_codes, ev_scales, tt, gain_d, spread, factors, out_groups = {}, {}, {}, {}, {}, {}, {}, {}, {}
 
         def transposes(c):
             ev_pairs = ev_rows[c].rearrange("p r k -> p (r k)").bitcast(F32)
@@ -120,8 +138,9 @@ def tile_generator_pa_e_kernel(tc, Pb, Ev, W_pie_words, W_pie_scales, feat, out)
                 )
 
         def products(c, r):
-            if r == 0:
-                gain_d[c] = work.tile([P, TILES], F32, name="gain_d")
+            g, cc = c // GROUP, c % GROUP
+            if cc == 0 and r == 0:
+                gain_d[g] = work.tile([P, GROUP, TILES], F32, name="gain_d")
             scratch = work.tile([P, ROW], F32, name="scratch")
             nc.vector.scalar_tensor_tensor(
                 out=scratch[:],
@@ -130,25 +149,50 @@ def tile_generator_pa_e_kernel(tc, Pb, Ev, W_pie_words, W_pie_scales, feat, out)
                 in1=pb_rows[c][:, r, :],
                 op0=MULT,
                 op1=MULT,
-                accum_out=gain_d[c][:, r : r + 1],
+                accum_out=gain_d[g][:, cc, r : r + 1],
             )
 
-        def make_factors(c):
-            factors[c] = work.tile([P, TILES], F32, name="factors")
-            nc.vector.tensor_scalar(out=factors[c][:], in0=gain_d[c][:], scalar1=1.0, scalar2=None, op0=ADD)
+        def spread_d(g):
+            spread[g] = work.tile([P, GROUP, GROUP, TILES], F32, name="spread")
+            nc.vector.tensor_tensor(
+                out=spread[g][:],
+                in0=gain_d[g][:].unsqueeze(2).to_broadcast([P, GROUP, GROUP, TILES]),
+                in1=at_part[:].unsqueeze(1).unsqueeze(3).to_broadcast([P, GROUP, GROUP, TILES]),
+                op=MULT,
+            )
 
-        def scale_and_store(c):
-            g, cc = c // GROUP, c % GROUP
-            if cc == 0:
-                out_groups[g] = resident.tile([P, GROUP, TILES, ROW], F32, name="out_g")
-            for r in range(TILES):
+        def move_d(g):
+            moved = psum_moved.tile([P, LONG], F32)
+            for cc in range(GROUP):
+                nc.tensor.matmul(
+                    out=moved[:],
+                    lhsT=carry[:, cc, :],
+                    rhs=spread[g][:, cc].rearrange("m e r -> m (e r)"),
+                    start=(cc == 0),
+                    stop=(cc == GROUP - 1),
+                )
+            factors[g] = work.tile([P, LONG], F32, name="factors")
+            nc.scalar.activation(out=factors[g][:], in_=moved[:], func=COPY, bias=1.0)
+
+        def scale(g, rows):
+            if rows[0] == 0:
+                out_groups[g] = resident.tile([P, LONG, ROW], F32, name="out_g")
+            for l in rows:
                 nc.scalar.activation(
-                    out=out_groups[g][:, cc, r, :], in_=feat_rows[c][:, r, :], func=COPY, scale=factors[c][:, r : r + 1]
+                    out=out_groups[g][:, l, :], in_=feat_rows[g][:, l, :], func=COPY, scale=factors[g][:, l : l + 1]
                 )
-            if cc == GROUP - 1:
-                nc.sync.dma_start(
-                    out=out[GROUP * g : GROUP * (g + 1)].rearrange("c (p r) n -> p c r n", r=TILES), in_=out_groups[g][:]
+
+        def scale_on_vector(g, rows):
+            for l in rows:
+                nc.vector.tensor_scalar(
+                    out=out_groups[g][:, l, :], in0=feat_rows[g][:, l, :], scalar1=factors[g][:, l : l + 1], scalar2=None, op0=MULT
                 )
+
+        def store(g):
+            nc.sync.dma_start(
+                out=out[GROUP * g : GROUP * (g + 1)].rearrange("c i n -> (c i) n").rearrange("(p l) n -> p l n", l=LONG),
+                in_=out_groups[g][:],
+            )
 
         def in_range(c):
             return 0 <= c < C
@@ -160,8 +204,11 @@ def tile_generator_pa_e_kernel(tc, Pb, Ev, W_pie_words, W_pie_scales, feat, out)
         reorder(0)
         quantise(0)
         for c in range(C + 1):
+            done = c // GROUP - 1
             if in_range(c):
                 passes(c)
+            if done >= 0 and c % GROUP == 0:
+                move_d(done)
             if in_range(c + 2):
                 transposes(c + 2)
             if in_range(c):
@@ -175,8 +222,15 @@ def tile_generator_pa_e_kernel(tc, Pb, Ev, W_pie_words, W_pie_scales, feat, out)
             if in_range(c):
                 products(c, 2)
                 products(c, 3)
-                make_factors(c)
-            if in_range(c - 1):
-                scale_and_store(c - 1)
+                if c % GROUP == GROUP - 1:
+                    spread_d(c // GROUP)
+            if 0 <= done < C // GROUP - 1:
+                scale(done, list(range(TILES * (c % GROUP), TILES * (c % GROUP + 1))))
+                if c % GROUP == GROUP - 1:
+                    store(done)
+            if c == C:
+                scale(done, list(range(LONG // 2)))
+                scale_on_vector(done, list(range(LONG // 2, LONG)))
+                store(done)
             if in_range(c + 2):
                 copies(c + 2)

@@ -35,6 +35,7 @@ def tile_generator_pa_e_kernel(tc, Pb, Ev, W_pie_words, W_pie_scales, feat, out)
     with ExitStack() as stack:
         stack.enter_context(tc.manual_schedule())
         const = stack.enter_context(tc.tile_pool(name="const", bufs=1))
+        by_community = stack.enter_context(tc.tile_pool(name="by_community", bufs=C))
         resident = stack.enter_context(tc.tile_pool(name="resident", bufs=C // GROUP))
         work = stack.enter_context(tc.tile_pool(name="work", bufs=2))
         psum_flip = stack.enter_context(tc.psum_pool(name="psum_flip", bufs=3))
@@ -61,37 +62,52 @@ def tile_generator_pa_e_kernel(tc, Pb, Ev, W_pie_words, W_pie_scales, feat, out)
         nc.vector.memset(carry[:], 0.0)
         for cc in range(GROUP):
             nc.vector.tensor_copy(out=carry[:, cc, SPAN * cc : SPAN * (cc + 1)], in_=in_span[:])
-        ev_rows, pb_rows, feat_rows = [], [], []
-        for g in range(C // GROUP):
-            cs = slice(GROUP * g, GROUP * (g + 1))
-            ev_g = resident.tile([P, GROUP, TILES, ROW], BF16)
-            nc.sync.dma_start(out=ev_g[:], in_=Ev[cs].rearrange("c (p r) k -> p c r k", r=TILES))
+        ev_rows, pb_rows, feat_rows = {}, {}, {}
+
+        def load_ev(c):
+            ev_rows[c] = by_community.tile([P, TILES, ROW], BF16, name="ev_c")
+            nc.sync.dma_start(out=ev_rows[c][:], in_=Ev[c].rearrange("(p r) k -> p r k", r=TILES))
+
+        def load_scales(a):
+            for quad in range(QUADRANTS):
+                nc.sync.dma_start(
+                    out=s_arrived[32 * quad : 32 * quad + 16, a, :].bitcast(I32),
+                    in_=W_pie_scales[PLANES * a : PLANES * (a + 1), 4 * quad : 4 * quad + 4, :].bitcast(I32),
+                )
+
+        def load_w(c):
             nc.sync.dma_start(
-                out=w_arrived[:, cs, :].bitcast(I32),
-                in_=W_pie_words[cs].rearrange("c p n t -> p c (n t)").bitcast(I32),
+                out=w_arrived[:, c, :].bitcast(I32), in_=W_pie_words[c].rearrange("p n t -> p (n t)").bitcast(I32)
             )
-            if (GROUP * g) % PLANES == 0:
-                a = GROUP * g // PLANES
-                for quad in range(QUADRANTS):
-                    nc.sync.dma_start(
-                        out=s_arrived[32 * quad : 32 * quad + 16, a, :].bitcast(I32),
-                        in_=W_pie_scales[PLANES * a : PLANES * (a + 1), 4 * quad : 4 * quad + 4, :].bitcast(I32),
-                    )
-            pb_g = resident.tile([P, GROUP, TILES, ROW], BF16)
-            nc.sync.dma_start(out=pb_g[:], in_=Pb[cs].rearrange("c (m r) j -> m c r j", r=TILES))
-            feat_g = resident.tile([P, LONG, ROW], BF16)
+
+        def load_pb(c):
+            pb_rows[c] = by_community.tile([P, TILES, ROW], BF16, name="pb_c")
+            nc.sync.dma_start(out=pb_rows[c][:], in_=Pb[c].rearrange("(m r) j -> m r j", r=TILES))
+
+        def load_feat(g):
+            feat_rows[g] = resident.tile([P, LONG, ROW], BF16, name="feat_g")
             nc.sync.dma_start(
-                out=feat_g[:], in_=feat[cs].rearrange("c i n -> (c i) n").rearrange("(p l) n -> p l n", l=LONG)
+                out=feat_rows[g][:],
+                in_=feat[GROUP * g : GROUP * (g + 1)].rearrange("c i n -> (c i) n").rearrange("(p l) n -> p l n", l=LONG),
             )
-            feat_rows.append(feat_g)
-            for cc in range(GROUP):
-                ev_rows.append(ev_g[:, cc])
-                pb_rows.append(pb_g[:, cc])
+
+        load_ev(0)
+        load_ev(1)
+        for c in range(C):
+            if c % PLANES == 0:
+                load_scales(c // PLANES)
+            load_w(c)
+            load_pb(c)
+            if c >= GROUP and c % GROUP == 0:
+                load_feat(c // GROUP - 1)
+            if c + 2 < C:
+                load_ev(c + 2)
+        load_feat(C // GROUP - 1)
 
         flipped, ev_kfirst, ev_codes, ev_scales, tt, gain_d, spread, factors, out_groups = {}, {}, {}, {}, {}, {}, {}, {}, {}
 
         def transposes(c):
-            ev_pairs = ev_rows[c].rearrange("p r k -> p (r k)").bitcast(F32)
+            ev_pairs = ev_rows[c][:].rearrange("p r k -> p (r k)").bitcast(F32)
             for half in range(2):
                 flipped[c, half] = psum_flip.tile([P, 4, P], F32, name="flipped")
                 for a in range(4):

@@ -205,7 +205,8 @@ def tile_generator_pa_e_kernel(tc, Pb, Ev, W_pie_words, W_pie_scales, feat, out)
                 )
 
         def store(g):
-            nc.sync.dma_start(
+            queue = nc.scalar if g % 2 == 0 else nc.sync
+            queue.dma_start(
                 out=out[GROUP * g : GROUP * (g + 1)].rearrange("c i n -> (c i) n").rearrange("(p l) n -> p l n", l=LONG),
                 in_=out_groups[g][:],
             )
@@ -221,6 +222,9 @@ def tile_generator_pa_e_kernel(tc, Pb, Ev, W_pie_words, W_pie_scales, feat, out)
         quantise(0)
         for c in range(C + 1):
             done = c // GROUP - 1
+            if c == C:
+                for g in range(0, C // GROUP - 1, 2):
+                    store(g)
             if in_range(c):
                 passes(c)
             if done >= 0 and c % GROUP == 0:
@@ -242,7 +246,7 @@ def tile_generator_pa_e_kernel(tc, Pb, Ev, W_pie_words, W_pie_scales, feat, out)
                     spread_d(c // GROUP)
             if 0 <= done < C // GROUP - 1:
                 scale(done, list(range(TILES * (c % GROUP), TILES * (c % GROUP + 1))))
-                if c % GROUP == GROUP - 1:
+                if c % GROUP == GROUP - 1 and done % 2 == 1:
                     store(done)
             if c == C:
                 scale(done, list(range(LONG // 2)))

@@ -22,6 +22,7 @@ TILES = ROW // P
 PAIRS = ROW // 2
 QUADRANTS = 4
 GAIN = 0.3
+LINE = 256
 GROUP = 2
 LONG = GROUP * TILES
 SPAN = P // GROUP
@@ -42,30 +43,30 @@ def tile_generator_pa_e_kernel(tc, Pb, Ev, W_pie_words, W_pie_scales, feat, out)
         psum_tt = stack.enter_context(tc.psum_pool(name="psum_tt", bufs=4))
         psum_moved = stack.enter_context(tc.psum_pool(name="psum_moved", bufs=1))
 
-        w_arrived = const.tile([P, C, ROW], U32)
-        w_codes = const.tile([P, C, ROW], U32, align_bytes=64)
-        s_arrived = const.tile([P, C // PLANES, ROW], U8)
+        w_arrived = const.tile([P, C, ROW], U32, align_bytes=LINE)
+        w_codes = const.tile([P, C, ROW], U32, align_bytes=LINE)
+        s_arrived = const.tile([P, C // PLANES, ROW], U8, align_bytes=LINE)
         nc.vector.memset(s_arrived[:].rearrange("p a n -> p (a n)").bitcast(I32), 0)
-        w_scales = const.tile([P, C // PLANES, ROW], U8, align_bytes=64)
+        w_scales = const.tile([P, C // PLANES, ROW], U8, align_bytes=LINE)
 
-        ident = const.tile([P, P], F32)
+        ident = const.tile([P, P], F32, align_bytes=LINE)
         make_identity(nc, ident[:])
-        in_span = const.tile([P, SPAN], F32)
+        in_span = const.tile([P, SPAN], F32, align_bytes=LINE)
         nc.vector.tensor_reduce(
             out=in_span[:], in_=ident[:].rearrange("m (b e) -> m b e", e=GROUP), axis=ALONG_ROW, op=ADD
         )
-        at_part = const.tile([P, GROUP], F32)
+        at_part = const.tile([P, GROUP], F32, align_bytes=LINE)
         nc.vector.tensor_reduce(
             out=at_part[:], in_=ident[:].rearrange("m (b e) -> m e b", e=GROUP), axis=ALONG_ROW, op=ADD
         )
-        carry = const.tile([P, GROUP, P], F32)
+        carry = const.tile([P, GROUP, P], F32, align_bytes=LINE)
         nc.vector.memset(carry[:], 0.0)
         for cc in range(GROUP):
             nc.vector.tensor_copy(out=carry[:, cc, SPAN * cc : SPAN * (cc + 1)], in_=in_span[:])
         ev_rows, pb_rows, feat_rows = {}, {}, {}
 
         def load_ev(c):
-            ev_rows[c] = by_community.tile([P, TILES, ROW], BF16, name="ev_c")
+            ev_rows[c] = by_community.tile([P, TILES, ROW], BF16, name="ev_c", align_bytes=LINE)
             nc.sync.dma_start(out=ev_rows[c][:], in_=Ev[c].rearrange("(p r) k -> p r k", r=TILES))
 
         def load_scales(a):
@@ -81,11 +82,11 @@ def tile_generator_pa_e_kernel(tc, Pb, Ev, W_pie_words, W_pie_scales, feat, out)
             )
 
         def load_pb(c):
-            pb_rows[c] = by_community.tile([P, TILES, ROW], BF16, name="pb_c")
+            pb_rows[c] = by_community.tile([P, TILES, ROW], BF16, name="pb_c", align_bytes=LINE)
             nc.sync.dma_start(out=pb_rows[c][:], in_=Pb[c].rearrange("(m r) j -> m r j", r=TILES))
 
         def load_feat(g):
-            feat_rows[g] = resident.tile([P, LONG, ROW], BF16, name="feat_g")
+            feat_rows[g] = resident.tile([P, LONG, ROW], BF16, name="feat_g", align_bytes=LINE)
             nc.sync.dma_start(
                 out=feat_rows[g][:],
                 in_=feat[GROUP * g : GROUP * (g + 1)].rearrange("c i n -> (c i) n").rearrange("(p l) n -> p l n", l=LONG),
@@ -117,14 +118,14 @@ def tile_generator_pa_e_kernel(tc, Pb, Ev, W_pie_words, W_pie_scales, feat, out)
                     )
 
         def copies(c):
-            ev_kfirst[c] = work.tile([P, ROW * PACK], BF16, name="ev_kfirst", align_bytes=64)
+            ev_kfirst[c] = work.tile([P, ROW * PACK], BF16, name="ev_kfirst", align_bytes=LINE)
             kfirst_pairs = ev_kfirst[c][:].bitcast(F32).rearrange("q (p half a) -> q p half a", half=2, a=4)
             for half in range(2):
                 nc.scalar.copy(out=kfirst_pairs[:, :, half, :], in_=flipped[c, half][:].rearrange("q a p -> q p a"))
 
         def quantise(c):
-            ev_codes[c] = work.tile([P, ROW], U32, name="ev_codes", align_bytes=64)
-            ev_scales[c] = work.tile([P, ROW], U8, name="ev_scales", align_bytes=64)
+            ev_codes[c] = work.tile([P, ROW], U32, name="ev_codes", align_bytes=LINE)
+            ev_scales[c] = work.tile([P, ROW], U8, name="ev_scales", align_bytes=LINE)
             nc.vector.quantize_mx(out=ev_codes[c][:].bitcast(FP8X4), scales=ev_scales[c][:], in_=ev_kfirst[c][:])
 
         def reorder_scales(a):
@@ -156,8 +157,8 @@ def tile_generator_pa_e_kernel(tc, Pb, Ev, W_pie_words, W_pie_scales, feat, out)
         def products(c, r):
             g, cc = c // GROUP, c % GROUP
             if cc == 0 and r == 0:
-                gain_d[g] = work.tile([P, GROUP, TILES], F32, name="gain_d")
-            scratch = work.tile([P, ROW], F32, name="scratch")
+                gain_d[g] = work.tile([P, GROUP, TILES], F32, name="gain_d", align_bytes=LINE)
+            scratch = work.tile([P, ROW], F32, name="scratch", align_bytes=LINE)
             nc.vector.scalar_tensor_tensor(
                 out=scratch[:],
                 in0=tt[c, r][:],
@@ -169,7 +170,7 @@ def tile_generator_pa_e_kernel(tc, Pb, Ev, W_pie_words, W_pie_scales, feat, out)
             )
 
         def spread_d(g):
-            spread[g] = work.tile([P, GROUP, GROUP, TILES], F32, name="spread")
+            spread[g] = work.tile([P, GROUP, GROUP, TILES], F32, name="spread", align_bytes=LINE)
             nc.vector.tensor_tensor(
                 out=spread[g][:],
                 in0=gain_d[g][:].unsqueeze(2).to_broadcast([P, GROUP, GROUP, TILES]),
@@ -187,12 +188,12 @@ def tile_generator_pa_e_kernel(tc, Pb, Ev, W_pie_words, W_pie_scales, feat, out)
                     start=(cc == 0),
                     stop=(cc == GROUP - 1),
                 )
-            factors[g] = work.tile([P, LONG], F32, name="factors")
+            factors[g] = work.tile([P, LONG], F32, name="factors", align_bytes=LINE)
             nc.scalar.activation(out=factors[g][:], in_=moved[:], func=COPY, bias=1.0)
 
         def scale(g, rows):
             if rows[0] == 0:
-                out_groups[g] = resident.tile([P, LONG, ROW], F32, name="out_g")
+                out_groups[g] = resident.tile([P, LONG, ROW], F32, name="out_g", align_bytes=LINE)
             for l in rows:
                 nc.scalar.activation(
                     out=out_groups[g][:, l, :], in_=feat_rows[g][:, l, :], func=COPY, scale=factors[g][:, l : l + 1]

@@ -38,6 +38,8 @@ def tile_generator_pa_e_kernel(tc, Pb, Ev, W_pie_words, W_pie_scales, feat, out)
         const = stack.enter_context(tc.tile_pool(name="const", bufs=1))
         by_community = stack.enter_context(tc.tile_pool(name="by_community", bufs=C))
         resident = stack.enter_context(tc.tile_pool(name="resident", bufs=C // GROUP))
+        table = stack.enter_context(tc.tile_pool(name="table", bufs=1))
+        stored = stack.enter_context(tc.tile_pool(name="stored", bufs=C // GROUP))
         work = stack.enter_context(tc.tile_pool(name="work", bufs=2))
         psum_flip = stack.enter_context(tc.psum_pool(name="psum_flip", bufs=3))
         psum_tt = stack.enter_context(tc.psum_pool(name="psum_tt", bufs=4))
@@ -55,7 +57,7 @@ def tile_generator_pa_e_kernel(tc, Pb, Ev, W_pie_words, W_pie_scales, feat, out)
         nc.vector.tensor_reduce(
             out=in_span[:], in_=ident[:].rearrange("m (b e) -> m b e", e=GROUP), axis=ALONG_ROW, op=ADD
         )
-        at_part = const.tile([P, GROUP], F32, align_bytes=LINE)
+        at_part = table.tile([P, GROUP], F32, align_bytes=LINE)
         nc.vector.tensor_reduce(
             out=at_part[:], in_=ident[:].rearrange("m (b e) -> m e b", e=GROUP), axis=ALONG_ROW, op=ADD
         )
@@ -193,7 +195,7 @@ def tile_generator_pa_e_kernel(tc, Pb, Ev, W_pie_words, W_pie_scales, feat, out)
 
         def scale(g, rows):
             if rows[0] == 0:
-                out_groups[g] = resident.tile([P, LONG, ROW], F32, name="out_g", align_bytes=LINE)
+                out_groups[g] = stored.tile([P, LONG, ROW], F32, name="out_g")
             for l in rows:
                 nc.scalar.activation(
                     out=out_groups[g][:, l, :], in_=feat_rows[g][:, l, :], func=COPY, scale=factors[g][:, l : l + 1]

@@ -36,7 +36,6 @@ def tile_generator_pa_e_kernel(tc, Pb, Ev, W_pie_words, W_pie_scales, feat, out)
     with ExitStack() as stack:
         stack.enter_context(tc.manual_schedule())
         const = stack.enter_context(tc.tile_pool(name="const", bufs=1))
-        by_community = stack.enter_context(tc.tile_pool(name="by_community", bufs=C))
         resident = stack.enter_context(tc.tile_pool(name="resident", bufs=C // GROUP))
         table = stack.enter_context(tc.tile_pool(name="table", bufs=1))
         stored = stack.enter_context(tc.tile_pool(name="stored", bufs=C // GROUP))
@@ -67,9 +66,11 @@ def tile_generator_pa_e_kernel(tc, Pb, Ev, W_pie_words, W_pie_scales, feat, out)
             nc.vector.tensor_copy(out=carry[:, cc, SPAN * cc : SPAN * (cc + 1)], in_=in_span[:])
         ev_rows, pb_rows, feat_rows = {}, {}, {}
 
-        def load_ev(c):
-            ev_rows[c] = by_community.tile([P, TILES, ROW], BF16, name="ev_c", align_bytes=LINE)
-            nc.sync.dma_start(out=ev_rows[c][:], in_=Ev[c].rearrange("(p r) k -> p r k", r=TILES))
+        def load_ev(first, n):
+            ev = const.tile([P, n, TILES, ROW], BF16, name="ev_%d" % first, align_bytes=LINE)
+            nc.sync.dma_start(out=ev[:], in_=Ev[first : first + n].rearrange("c (p r) k -> p c r k", r=TILES))
+            for cc in range(n):
+                ev_rows[first + cc] = ev[:, cc]
 
         def load_scales(a):
             for quad in range(QUADRANTS):
@@ -78,14 +79,17 @@ def tile_generator_pa_e_kernel(tc, Pb, Ev, W_pie_words, W_pie_scales, feat, out)
                     in_=W_pie_scales[PLANES * a : PLANES * (a + 1), 4 * quad : 4 * quad + 4, :].bitcast(I32),
                 )
 
-        def load_w(c):
+        def load_w(first, n):
             nc.sync.dma_start(
-                out=w_arrived[:, c, :].bitcast(I32), in_=W_pie_words[c].rearrange("p n t -> p (n t)").bitcast(I32)
+                out=w_arrived[:, first : first + n, :].bitcast(I32),
+                in_=W_pie_words[first : first + n].rearrange("c p n t -> p c (n t)").bitcast(I32),
             )
 
-        def load_pb(c):
-            pb_rows[c] = by_community.tile([P, TILES, ROW], BF16, name="pb_c", align_bytes=LINE)
-            nc.sync.dma_start(out=pb_rows[c][:], in_=Pb[c].rearrange("(m r) j -> m r j", r=TILES))
+        def load_pb(first, n):
+            pb = const.tile([P, n, TILES, ROW], BF16, name="pb_%d" % first, align_bytes=LINE)
+            nc.sync.dma_start(out=pb[:], in_=Pb[first : first + n].rearrange("c (m r) j -> m c r j", r=TILES))
+            for cc in range(n):
+                pb_rows[first + cc] = pb[:, cc]
 
         def load_feat(g):
             feat_rows[g] = resident.tile([P, LONG, ROW], BF16, name="feat_g", align_bytes=LINE)
@@ -94,23 +98,31 @@ def tile_generator_pa_e_kernel(tc, Pb, Ev, W_pie_words, W_pie_scales, feat, out)
                 in_=feat[GROUP * g : GROUP * (g + 1)].rearrange("c i n -> (c i) n").rearrange("(p l) n -> p l n", l=LONG),
             )
 
-        load_ev(0)
-        load_ev(1)
-        for c in range(C):
-            if c % PLANES == 0:
-                load_scales(c // PLANES)
-            load_w(c)
-            load_pb(c)
-            if c >= GROUP and c % GROUP == 0:
-                load_feat(c // GROUP - 1)
-            if c + 2 < C:
-                load_ev(c + 2)
-        load_feat(C // GROUP - 1)
+        load_ev(0, 1)
+        load_scales(0)
+        load_w(0, 2)
+        load_ev(1, 1)
+        load_pb(0, 2)
+        load_ev(2, 1)
+        load_ev(3, 1)
+        load_w(2, 2)
+        load_pb(2, 2)
+        load_ev(4, 2)
+        load_feat(0)
+        load_scales(1)
+        load_w(4, 2)
+        load_pb(4, 2)
+        load_ev(6, 2)
+        load_feat(1)
+        for c in (6, 7):
+            load_w(c, 1)
+            load_pb(c, 1)
+            load_feat(c - 4)
 
         flipped, ev_kfirst, ev_codes, ev_scales, tt, gain_d, spread, factors, out_groups = {}, {}, {}, {}, {}, {}, {}, {}, {}
 
         def transposes(c):
-            ev_pairs = ev_rows[c][:].rearrange("p r k -> p (r k)").bitcast(F32)
+            ev_pairs = ev_rows[c].rearrange("p r k -> p (r k)").bitcast(F32)
             for half in range(2):
                 flipped[c, half] = psum_flip.tile([P, 4, P], F32, name="flipped")
                 for a in range(4):

@@ -9,24 +9,24 @@ I32 = mybir.dt.int32
 U32 = mybir.dt.uint32
 U8 = mybir.dt.uint8
 FP8X4 = mybir.dt.float8_e4m3fn_x4
-ADD = mybir.AluOpType.add
 MULT = mybir.AluOpType.mult
-ALONG_ROW = mybir.AxisListType.X
 COPY = mybir.ActivationFunctionType.Copy
 
 P = 128
 PACK = 4
 C = 8
 ROW = 512
-TILES = ROW // P
-PAIRS = ROW // 2
+GROUP = 2
+PAIRS = C // GROUP
+SPAN = P // GROUP
+LONG = GROUP * ROW // P
+WORDS = ROW // 2
+BANKS = 4
+FLIPS = 4
 QUADRANTS = 4
+PLANES = 4
 GAIN = 0.3
 LINE = 256
-GROUP = 2
-LONG = GROUP * TILES
-SPAN = P // GROUP
-PLANES = 4
 
 FLOPS = C * (2 * ROW * ROW * ROW + 2 * ROW * ROW + 3 * ROW * ROW)
 
@@ -36,41 +36,31 @@ def tile_generator_pa_e_kernel(tc, Pb, Ev, W_pie_words, W_pie_scales, feat, out)
     with ExitStack() as stack:
         stack.enter_context(tc.manual_schedule())
         const = stack.enter_context(tc.tile_pool(name="const", bufs=1))
-        resident = stack.enter_context(tc.tile_pool(name="resident", bufs=C // GROUP))
-        table = stack.enter_context(tc.tile_pool(name="table", bufs=1))
-        stored = stack.enter_context(tc.tile_pool(name="stored", bufs=C // GROUP))
+        resident = stack.enter_context(tc.tile_pool(name="resident", bufs=PAIRS))
         work = stack.enter_context(tc.tile_pool(name="work", bufs=2))
-        psum_flip = stack.enter_context(tc.psum_pool(name="psum_flip", bufs=3))
+        psum_flip = stack.enter_context(tc.psum_pool(name="psum_flip", bufs=BANKS))
         psum_tt = stack.enter_context(tc.psum_pool(name="psum_tt", bufs=4))
-        psum_moved = stack.enter_context(tc.psum_pool(name="psum_moved", bufs=1))
 
         w_arrived = const.tile([P, C, ROW], U32, align_bytes=LINE)
-        w_codes = const.tile([P, C, ROW], U32, align_bytes=LINE)
+        w_codes = const.tile([P, PAIRS, LONG, 3 * SPAN], U32, align_bytes=LINE)
         s_arrived = const.tile([P, C // PLANES, ROW], U8, align_bytes=LINE)
         nc.vector.memset(s_arrived[:].rearrange("p a n -> p (a n)").bitcast(I32), 0)
-        w_scales = const.tile([P, C // PLANES, ROW], U8, align_bytes=LINE)
+        w_scales = const.tile([P, C // PLANES, (LONG + 2) * SPAN], U8, align_bytes=LINE)
+        nc.vector.memset(w_scales[:].rearrange("p a n -> p (a n)").bitcast(I32), 0)
 
         ident = const.tile([P, P], F32, align_bytes=LINE)
         make_identity(nc, ident[:])
-        in_span = const.tile([P, SPAN], F32, align_bytes=LINE)
-        nc.vector.tensor_reduce(
-            out=in_span[:], in_=ident[:].rearrange("m (b e) -> m b e", e=GROUP), axis=ALONG_ROW, op=ADD
-        )
-        at_part = table.tile([P, GROUP], F32, align_bytes=LINE)
-        nc.vector.tensor_reduce(
-            out=at_part[:], in_=ident[:].rearrange("m (b e) -> m e b", e=GROUP), axis=ALONG_ROW, op=ADD
-        )
-        carry = const.tile([P, GROUP, P], F32, align_bytes=LINE)
-        nc.vector.memset(carry[:], 0.0)
-        for cc in range(GROUP):
-            nc.vector.tensor_copy(out=carry[:, cc, SPAN * cc : SPAN * (cc + 1)], in_=in_span[:])
+        nc.gpsimd.memset(w_codes[:, :, :, SPAN : 2 * SPAN], 0)
+
         ev_rows, pb_rows, feat_rows = {}, {}, {}
 
-        def load_ev(first, n):
-            ev = const.tile([P, n, TILES, ROW], BF16, name="ev_%d" % first, align_bytes=LINE)
-            nc.sync.dma_start(out=ev[:], in_=Ev[first : first + n].rearrange("c (p r) k -> p c r k", r=TILES))
-            for cc in range(n):
-                ev_rows[first + cc] = ev[:, cc]
+        def pair_rows(matrix, g):
+            return matrix[GROUP * g : GROUP * (g + 1)].rearrange("c i n -> (c i) n").rearrange("(p l) n -> p l n", l=LONG)
+
+        def load_rows(matrix, g, name):
+            rows = resident.tile([P, LONG, ROW], BF16, name=name, align_bytes=LINE)
+            nc.sync.dma_start(out=rows[:], in_=pair_rows(matrix, g))
+            return rows
 
         def load_scales(a):
             for quad in range(QUADRANTS):
@@ -79,193 +69,189 @@ def tile_generator_pa_e_kernel(tc, Pb, Ev, W_pie_words, W_pie_scales, feat, out)
                     in_=W_pie_scales[PLANES * a : PLANES * (a + 1), 4 * quad : 4 * quad + 4, :].bitcast(I32),
                 )
 
-        def load_w(first, n):
+        def load_w(g):
+            pair = slice(GROUP * g, GROUP * (g + 1))
             nc.sync.dma_start(
-                out=w_arrived[:, first : first + n, :].bitcast(I32),
-                in_=W_pie_words[first : first + n].rearrange("c p n t -> p c (n t)").bitcast(I32),
+                out=w_arrived[:, pair, :].bitcast(I32),
+                in_=W_pie_words[pair].rearrange("c p n t -> p c (n t)").bitcast(I32),
             )
 
-        def load_pb(first, n):
-            pb = const.tile([P, n, TILES, ROW], BF16, name="pb_%d" % first, align_bytes=LINE)
-            nc.sync.dma_start(out=pb[:], in_=Pb[first : first + n].rearrange("c (m r) j -> m c r j", r=TILES))
-            for cc in range(n):
-                pb_rows[first + cc] = pb[:, cc]
+        def load_ev(g):
+            ev_rows[g] = load_rows(Ev, g, "ev_g")
+
+        def load_half_ev(g, half):
+            if half == 0:
+                ev_rows[g] = resident.tile([P, LONG, ROW], BF16, name="ev_g", align_bytes=LINE)
+            rows = slice(LONG // 2 * half, LONG // 2 * (half + 1))
+            nc.sync.dma_start(out=ev_rows[g][:, rows, :], in_=pair_rows(Ev, g)[:, rows, :])
+
+        def load_pb(g):
+            pb_rows[g] = load_rows(Pb, g, "pb_g")
 
         def load_feat(g):
-            feat_rows[g] = resident.tile([P, LONG, ROW], BF16, name="feat_g", align_bytes=LINE)
-            nc.sync.dma_start(
-                out=feat_rows[g][:],
-                in_=feat[GROUP * g : GROUP * (g + 1)].rearrange("c i n -> (c i) n").rearrange("(p l) n -> p l n", l=LONG),
-            )
+            feat_rows[g] = load_rows(feat, g, "feat_g")
 
-        load_ev(0, 1)
+        load_half_ev(0, 0)
         load_scales(0)
-        load_w(0, 2)
-        load_ev(1, 1)
-        load_pb(0, 2)
-        load_ev(2, 1)
-        load_ev(3, 1)
-        load_w(2, 2)
-        load_pb(2, 2)
-        load_ev(4, 2)
+        load_half_ev(0, 1)
+        load_w(0)
+        load_pb(0)
+        load_ev(1)
+        load_w(1)
+        load_ev(2)
+        load_pb(1)
         load_feat(0)
         load_scales(1)
-        load_w(4, 2)
-        load_pb(4, 2)
-        load_ev(6, 2)
+        load_w(2)
+        load_ev(3)
+        load_pb(2)
         load_feat(1)
-        for c in (6, 7):
-            load_w(c, 1)
-            load_pb(c, 1)
-            load_feat(c - 4)
+        load_w(3)
+        load_pb(3)
+        load_feat(2)
+        load_feat(3)
 
-        flipped, ev_kfirst, ev_codes, ev_scales, tt, gain_d, spread, factors, out_groups = {}, {}, {}, {}, {}, {}, {}, {}, {}
+        flipped, ev_kfirst, ev_codes, ev_scales, tt, gain_d, factors, out_rows = {}, {}, {}, {}, {}, {}, {}, {}
 
-        def transposes(c):
-            ev_pairs = ev_rows[c].rearrange("p r k -> p (r k)").bitcast(F32)
-            for half in range(2):
-                flipped[c, half] = psum_flip.tile([P, 4, P], F32, name="flipped")
-                for a in range(4):
-                    r, u = 2 * half + a // 2, a % 2
+        def transposes(g, half):
+            ev_words = ev_rows[g][:].rearrange("p l k -> p (l k)").bitcast(F32)
+            for b in range(BANKS // 2 * half, BANKS // 2 * (half + 1)):
+                flipped[g, b] = psum_flip.tile([P, FLIPS, P], F32, name="flipped")
+                for a in range(FLIPS):
+                    l, u = 2 * b + a // 2, a % 2
                     nc.tensor.transpose(
-                        flipped[c, half][:, a, :], ev_pairs[:, PAIRS * r + u : PAIRS * (r + 1) : 2], ident[:]
+                        flipped[g, b][:, a, :], ev_words[:, WORDS * l + u : WORDS * (l + 1) : 2], ident[:]
                     )
 
-        def copies(c):
-            ev_kfirst[c] = work.tile([P, ROW * PACK], BF16, name="ev_kfirst", align_bytes=LINE)
-            kfirst_pairs = ev_kfirst[c][:].bitcast(F32).rearrange("q (p half a) -> q p half a", half=2, a=4)
-            for half in range(2):
-                nc.scalar.copy(out=kfirst_pairs[:, :, half, :], in_=flipped[c, half][:].rearrange("q a p -> q p a"))
+        def copies(g, half):
+            if half == 0:
+                ev_kfirst[g] = work.tile([P, GROUP * ROW * PACK], BF16, name="ev_kfirst", align_bytes=LINE)
+            kfirst_words = ev_kfirst[g][:].bitcast(F32).rearrange("q (p b a) -> q p b a", b=BANKS, a=FLIPS)
+            for b in range(BANKS // 2 * half, BANKS // 2 * (half + 1)):
+                nc.scalar.copy(out=kfirst_words[:, :, b, :], in_=flipped[g, b][:].rearrange("q a p -> q p a"))
 
-        def quantise(c):
-            ev_codes[c] = work.tile([P, ROW], U32, name="ev_codes", align_bytes=LINE)
-            ev_scales[c] = work.tile([P, ROW], U8, name="ev_scales", align_bytes=LINE)
-            nc.vector.quantize_mx(out=ev_codes[c][:].bitcast(FP8X4), scales=ev_scales[c][:], in_=ev_kfirst[c][:])
+        def quantise(g, cc):
+            if cc == 0:
+                ev_codes[g] = work.tile([P, GROUP, ROW], U32, name="ev_codes", align_bytes=LINE)
+                ev_scales[g] = work.tile([P, GROUP, ROW], U8, name="ev_scales", align_bytes=LINE)
+            nc.vector.quantize_mx(
+                out=ev_codes[g][:, cc, :].bitcast(FP8X4),
+                scales=ev_scales[g][:, cc, :],
+                in_=ev_kfirst[g][:, ROW * PACK * cc : ROW * PACK * (cc + 1)],
+            )
 
         def reorder_scales(a):
-            nc.vector.tensor_copy(
-                out=w_scales[:, a, :].rearrange("p (r m) -> p m r", r=TILES),
-                in_=s_arrived[:, a, :].rearrange("p (m r) -> p m r", r=TILES),
-            )
-
-        def reorder(c):
-            nc.vector.tensor_copy(
-                out=w_codes[:, c, :].bitcast(I32).rearrange("p (r m) -> p r m", r=TILES),
-                in_=w_arrived[:, c, :].bitcast(I32).rearrange("p (m r) -> p r m", r=TILES),
-            )
-
-        def passes(c):
-            for r in range(TILES):
-                i_cols = slice(P * r, P * (r + 1))
-                tt[c, r] = psum_tt.tile([P, ROW], F32, name="tt")
-                nc.tensor.matmul_mx(
-                    out=tt[c, r][:],
-                    lhsT=w_codes[:, c, i_cols].bitcast(FP8X4),
-                    lhsT_scale=w_scales[4 * (c % PLANES) : P, c // PLANES, i_cols],
-                    rhs=ev_codes[c][:].bitcast(FP8X4),
-                    rhs_scale=ev_scales[c][:],
-                    start=True,
-                    stop=True,
+            for half in range(2):
+                first = SPAN + LONG // 2 * SPAN * half
+                nc.vector.tensor_copy(
+                    out=w_scales[:, a, first : first + LONG // 2 * SPAN].rearrange("p (r m) -> p m r", r=LONG // 2),
+                    in_=s_arrived[:, a, :].rearrange("p (m h r) -> p h m r", h=2, r=LONG // 2)[:, half],
                 )
 
-        def products(c, r):
-            g, cc = c // GROUP, c % GROUP
-            if cc == 0 and r == 0:
-                gain_d[g] = work.tile([P, GROUP, TILES], F32, name="gain_d", align_bytes=LINE)
-            scratch = work.tile([P, ROW], F32, name="scratch", align_bytes=LINE)
-            nc.vector.scalar_tensor_tensor(
-                out=scratch[:],
-                in0=tt[c, r][:],
-                scalar=GAIN,
-                in1=pb_rows[c][:, r, :],
-                op0=MULT,
-                op1=MULT,
-                accum_out=gain_d[g][:, cc, r : r + 1],
+        def reorder(g, cc):
+            nc.vector.tensor_copy(
+                out=w_codes[:, g, :, 2 * SPAN * cc : 2 * SPAN * cc + SPAN].bitcast(I32),
+                in_=w_arrived[:, GROUP * g + cc, :].bitcast(I32).rearrange("p (m r) -> p r m", r=LONG),
             )
 
-        def spread_d(g):
-            spread[g] = work.tile([P, GROUP, GROUP, TILES], F32, name="spread", align_bytes=LINE)
-            nc.vector.tensor_tensor(
-                out=spread[g][:],
-                in0=gain_d[g][:].unsqueeze(2).to_broadcast([P, GROUP, GROUP, TILES]),
-                in1=at_part[:].unsqueeze(1).unsqueeze(3).to_broadcast([P, GROUP, GROUP, TILES]),
-                op=MULT,
-            )
-
-        def move_d(g):
-            moved = psum_moved.tile([P, LONG], F32)
+        def passes(g, r):
+            tt[g, r] = psum_tt.tile([P, ROW], F32, name="tt")
             for cc in range(GROUP):
-                nc.tensor.matmul(
-                    out=moved[:],
-                    lhsT=carry[:, cc, :],
-                    rhs=spread[g][:, cc].rearrange("m e r -> m (e r)"),
+                c = GROUP * g + cc
+                first = SPAN * cc
+                nc.tensor.matmul_mx(
+                    out=tt[g, r][:],
+                    lhsT=w_codes[:, g, r, first : first + P].bitcast(FP8X4),
+                    lhsT_scale=w_scales[4 * (c % PLANES) : P, c // PLANES, SPAN * (r + 1) - first : SPAN * (r + 1) - first + P],
+                    rhs=ev_codes[g][:, cc, :].bitcast(FP8X4),
+                    rhs_scale=ev_scales[g][:, cc, :],
                     start=(cc == 0),
                     stop=(cc == GROUP - 1),
                 )
+
+        def products(g, r):
+            if r == 0:
+                gain_d[g] = work.tile([P, LONG], F32, name="gain_d", align_bytes=LINE)
+            scratch = work.tile([P, ROW], F32, name="scratch", align_bytes=LINE)
+            nc.vector.scalar_tensor_tensor(
+                out=scratch[:],
+                in0=tt[g, r][:],
+                scalar=GAIN,
+                in1=pb_rows[g][:, r, :],
+                op0=MULT,
+                op1=MULT,
+                accum_out=gain_d[g][:, r : r + 1],
+            )
+
+        def make_factors(g):
             factors[g] = work.tile([P, LONG], F32, name="factors", align_bytes=LINE)
-            nc.scalar.activation(out=factors[g][:], in_=moved[:], func=COPY, bias=1.0)
+            nc.scalar.activation(out=factors[g][:], in_=gain_d[g][:], func=COPY, bias=1.0)
+            out_rows[g] = resident.tile([P, LONG, ROW], F32, name="out_g", align_bytes=LINE)
 
         def scale(g, rows):
-            if rows[0] == 0:
-                out_groups[g] = stored.tile([P, LONG, ROW], F32, name="out_g")
             for l in rows:
                 nc.scalar.activation(
-                    out=out_groups[g][:, l, :], in_=feat_rows[g][:, l, :], func=COPY, scale=factors[g][:, l : l + 1]
+                    out=out_rows[g][:, l, :], in_=feat_rows[g][:, l, :], func=COPY, scale=factors[g][:, l : l + 1]
                 )
 
         def scale_on_vector(g, rows):
             for l in rows:
                 nc.vector.tensor_scalar(
-                    out=out_groups[g][:, l, :], in0=feat_rows[g][:, l, :], scalar1=factors[g][:, l : l + 1], scalar2=None, op0=MULT
+                    out=out_rows[g][:, l, :], in0=feat_rows[g][:, l, :], scalar1=factors[g][:, l : l + 1], scalar2=None, op0=MULT
                 )
 
-        def store(g):
-            queue = nc.scalar if g % 2 == 0 else nc.sync
-            queue.dma_start(
-                out=out[GROUP * g : GROUP * (g + 1)].rearrange("c i n -> (c i) n").rearrange("(p l) n -> p l n", l=LONG),
-                in_=out_groups[g][:],
-            )
+        def store(queue, g):
+            queue.dma_start(out=pair_rows(out, g), in_=out_rows[g][:])
 
-        def in_range(c):
-            return 0 <= c < C
-
-        for c in range(2):
-            transposes(c)
-            copies(c)
+        HALF = LONG // 2
+        for half in range(2):
+            transposes(0, half)
+            copies(0, half)
         reorder_scales(0)
-        reorder(0)
-        quantise(0)
-        for c in range(C + 1):
-            done = c // GROUP - 1
-            if c == C:
-                for g in range(0, C // GROUP - 1, 2):
-                    store(g)
-            if in_range(c):
-                passes(c)
-            if done >= 0 and c % GROUP == 0:
-                move_d(done)
-            if in_range(c + 2):
-                transposes(c + 2)
-            if in_range(c):
-                products(c, 0)
-                products(c, 1)
-            if in_range(c + 1):
-                if (c + 1) % PLANES == 0:
-                    reorder_scales((c + 1) // PLANES)
-                reorder(c + 1)
-                quantise(c + 1)
-            if in_range(c):
-                products(c, 2)
-                products(c, 3)
-                if c % GROUP == GROUP - 1:
-                    spread_d(c // GROUP)
-            if 0 <= done < C // GROUP - 1:
-                scale(done, list(range(TILES * (c % GROUP), TILES * (c % GROUP + 1))))
-                if c % GROUP == GROUP - 1 and done % 2 == 1:
-                    store(done)
-            if c == C:
-                scale(done, list(range(LONG // 2)))
-                scale_on_vector(done, list(range(LONG // 2, LONG)))
-                store(done)
-            if in_range(c + 2):
-                copies(c + 2)
+        for cc in range(GROUP):
+            reorder(0, cc)
+        for cc in range(GROUP):
+            quantise(0, cc)
+        for g in range(PAIRS):
+            more = g + 1 < PAIRS
+            for r in range(HALF):
+                passes(g, r)
+            if g == 0:
+                transposes(1, 0)
+            if more:
+                transposes(g + 1, 1)
+            if g > 0:
+                make_factors(g - 1)
+                scale(g - 1, range(3))
+            if g == 0:
+                copies(1, 0)
+            if more:
+                copies(g + 1, 1)
+            for r in range(HALF):
+                products(g, r)
+            if more:
+                if (GROUP * (g + 1)) % PLANES == 0:
+                    reorder_scales(GROUP * (g + 1) // PLANES)
+                for cc in range(GROUP):
+                    reorder(g + 1, cc)
+                quantise(g + 1, 0)
+            for r in range(HALF, LONG):
+                passes(g, r)
+            if g + 2 < PAIRS:
+                transposes(g + 2, 0)
+            for r in range(HALF, HALF + 2):
+                products(g, r)
+            if more:
+                quantise(g + 1, 1)
+            for r in range(HALF + 2, LONG):
+                products(g, r)
+            if g > 0:
+                scale(g - 1, range(3, LONG))
+                store(nc.scalar if g == PAIRS - 1 else nc.sync, g - 1)
+            if g + 2 < PAIRS:
+                copies(g + 2, 0)
+        last = PAIRS - 1
+        make_factors(last)
+        scale(last, range(3))
+        scale_on_vector(last, range(3, LONG))
+        store(nc.sync, last)

@@ -21,7 +21,8 @@ PAIRS = C // GROUP
 SPAN = P // GROUP
 LONG = GROUP * ROW // P
 WORDS = ROW // 2
-BANKS = 4
+TILES = ROW // P
+BANKS = 2
 FLIPS = 4
 QUADRANTS = 4
 PLANES = 4
@@ -36,9 +37,10 @@ def tile_generator_pa_e_kernel(tc, Pb, Ev, W_pie_words, W_pie_scales, feat, out)
     with ExitStack() as stack:
         stack.enter_context(tc.manual_schedule())
         const = stack.enter_context(tc.tile_pool(name="const", bufs=1))
+        by_community = stack.enter_context(tc.tile_pool(name="by_community", bufs=C))
         resident = stack.enter_context(tc.tile_pool(name="resident", bufs=PAIRS))
         work = stack.enter_context(tc.tile_pool(name="work", bufs=2))
-        psum_flip = stack.enter_context(tc.psum_pool(name="psum_flip", bufs=BANKS))
+        psum_flip = stack.enter_context(tc.psum_pool(name="psum_flip", bufs=GROUP * BANKS))
         psum_tt = stack.enter_context(tc.psum_pool(name="psum_tt", bufs=4))
 
         w_arrived = const.tile([P, C, ROW], U32, align_bytes=LINE)
@@ -76,14 +78,9 @@ def tile_generator_pa_e_kernel(tc, Pb, Ev, W_pie_words, W_pie_scales, feat, out)
                 in_=W_pie_words[pair].rearrange("c p n t -> p c (n t)").bitcast(I32),
             )
 
-        def load_ev(g):
-            ev_rows[g] = load_rows(Ev, g, "ev_g")
-
-        def load_half_ev(g, half):
-            if half == 0:
-                ev_rows[g] = resident.tile([P, LONG, ROW], BF16, name="ev_g", align_bytes=LINE)
-            rows = slice(LONG // 2 * half, LONG // 2 * (half + 1))
-            nc.sync.dma_start(out=ev_rows[g][:, rows, :], in_=pair_rows(Ev, g)[:, rows, :])
+        def load_ev(c):
+            ev_rows[c] = by_community.tile([P, TILES, ROW], BF16, name="ev_c", align_bytes=LINE)
+            nc.sync.dma_start(out=ev_rows[c][:], in_=Ev[c].rearrange("(p r) k -> p r k", r=TILES))
 
         def load_pb(g):
             pb_rows[g] = load_rows(Pb, g, "pb_g")
@@ -91,21 +88,24 @@ def tile_generator_pa_e_kernel(tc, Pb, Ev, W_pie_words, W_pie_scales, feat, out)
         def load_feat(g):
             feat_rows[g] = load_rows(feat, g, "feat_g")
 
-        load_half_ev(0, 0)
+        load_ev(0)
         load_scales(0)
-        load_half_ev(0, 1)
         load_w(0)
-        load_pb(0)
         load_ev(1)
-        load_w(1)
+        load_pb(0)
         load_ev(2)
+        load_ev(3)
+        load_w(1)
         load_pb(1)
+        load_ev(4)
         load_feat(0)
+        load_ev(5)
         load_scales(1)
         load_w(2)
-        load_ev(3)
         load_pb(2)
+        load_ev(6)
         load_feat(1)
+        load_ev(7)
         load_w(3)
         load_pb(3)
         load_feat(2)
@@ -113,22 +113,22 @@ def tile_generator_pa_e_kernel(tc, Pb, Ev, W_pie_words, W_pie_scales, feat, out)
 
         flipped, ev_kfirst, ev_codes, ev_scales, tt, gain_d, factors, out_rows = {}, {}, {}, {}, {}, {}, {}, {}
 
-        def transposes(g, half):
-            ev_words = ev_rows[g][:].rearrange("p l k -> p (l k)").bitcast(F32)
-            for b in range(BANKS // 2 * half, BANKS // 2 * (half + 1)):
-                flipped[g, b] = psum_flip.tile([P, FLIPS, P], F32, name="flipped")
+        def transposes(g, cc):
+            ev_words = ev_rows[GROUP * g + cc][:].rearrange("p r k -> p (r k)").bitcast(F32)
+            for b in range(BANKS):
+                flipped[g, cc, b] = psum_flip.tile([P, FLIPS, P], F32, name="flipped")
                 for a in range(FLIPS):
-                    l, u = 2 * b + a // 2, a % 2
+                    r, u = 2 * b + a // 2, a % 2
                     nc.tensor.transpose(
-                        flipped[g, b][:, a, :], ev_words[:, WORDS * l + u : WORDS * (l + 1) : 2], ident[:]
+                        flipped[g, cc, b][:, a, :], ev_words[:, WORDS * r + u : WORDS * (r + 1) : 2], ident[:]
                     )
 
-        def copies(g, half):
-            if half == 0:
-                ev_kfirst[g] = work.tile([P, GROUP * ROW * PACK], BF16, name="ev_kfirst", align_bytes=LINE)
-            kfirst_words = ev_kfirst[g][:].bitcast(F32).rearrange("q (p b a) -> q p b a", b=BANKS, a=FLIPS)
-            for b in range(BANKS // 2 * half, BANKS // 2 * (half + 1)):
-                nc.scalar.copy(out=kfirst_words[:, :, b, :], in_=flipped[g, b][:].rearrange("q a p -> q p a"))
+        def copies(g, cc):
+            if cc == 0:
+                ev_kfirst[g] = work.tile([P, GROUP, ROW * PACK], BF16, name="ev_kfirst", align_bytes=LINE)
+            kfirst_words = ev_kfirst[g][:, cc, :].bitcast(F32).rearrange("q (p b a) -> q p b a", b=BANKS, a=FLIPS)
+            for b in range(BANKS):
+                nc.scalar.copy(out=kfirst_words[:, :, b, :], in_=flipped[g, cc, b][:].rearrange("q a p -> q p a"))
 
         def quantise(g, cc):
             if cc == 0:
@@ -137,7 +137,7 @@ def tile_generator_pa_e_kernel(tc, Pb, Ev, W_pie_words, W_pie_scales, feat, out)
             nc.vector.quantize_mx(
                 out=ev_codes[g][:, cc, :].bitcast(FP8X4),
                 scales=ev_scales[g][:, cc, :],
-                in_=ev_kfirst[g][:, ROW * PACK * cc : ROW * PACK * (cc + 1)],
+                in_=ev_kfirst[g][:, cc, :],
             )
 
         def reorder_scales(a):
@@ -223,6 +223,8 @@ def tile_generator_pa_e_kernel(tc, Pb, Ev, W_pie_words, W_pie_scales, feat, out)
             if g > 0:
                 make_factors(g - 1)
                 scale(g - 1, range(3))
+            if g == PAIRS - 1:
+                store(nc.scalar, 0)
             if g == 0:
                 copies(1, 0)
             if more:
@@ -247,7 +249,10 @@ def tile_generator_pa_e_kernel(tc, Pb, Ev, W_pie_words, W_pie_scales, feat, out)
                 products(g, r)
             if g > 0:
                 scale(g - 1, range(3, LONG))
-                store(nc.scalar if g == PAIRS - 1 else nc.sync, g - 1)
+                if g == 2:
+                    store(nc.sync, 1)
+                if g == PAIRS - 1:
+                    store(nc.scalar, 2)
             if g + 2 < PAIRS:
                 copies(g + 2, 0)
         last = PAIRS - 1

from contextlib import ExitStack

import concourse.mybir as mybir
from concourse.masks import make_identity

F32 = mybir.dt.float32
BF16 = mybir.dt.bfloat16
I32 = mybir.dt.int32
U32 = mybir.dt.uint32
U8 = mybir.dt.uint8
FP8X4 = mybir.dt.float8_e4m3fn_x4
MULT = mybir.AluOpType.mult
COPY = mybir.ActivationFunctionType.Copy

P = 128
PACK = 4
C = 8
ROW = 512
GROUP = 2
PAIRS = C // GROUP
SPAN = P // GROUP
LONG = GROUP * ROW // P
WORDS = ROW // 2
TILES = ROW // P
BANKS = 2
FLIPS = 4
QUADRANTS = 4
PLANES = 4
GAIN = 0.3
LINE = 256

FLOPS = C * (2 * ROW * ROW * ROW + 2 * ROW * ROW + 3 * ROW * ROW)


def tile_generator_pa_e_kernel(tc, Pb, Ev, W_pie_words, W_pie_scales, feat, out):
    nc = tc.nc
    with ExitStack() as stack:
        stack.enter_context(tc.manual_schedule())
        const = stack.enter_context(tc.tile_pool(name="const", bufs=1))
        by_community = stack.enter_context(tc.tile_pool(name="by_community", bufs=C))
        resident = stack.enter_context(tc.tile_pool(name="resident", bufs=PAIRS))
        work = stack.enter_context(tc.tile_pool(name="work", bufs=2))
        psum_flip = stack.enter_context(tc.psum_pool(name="psum_flip", bufs=GROUP * BANKS))
        psum_tt = stack.enter_context(tc.psum_pool(name="psum_tt", bufs=4))

        w_arrived = const.tile([P, C, ROW], U32, align_bytes=LINE)
        w_codes = const.tile([P, PAIRS, LONG, 3 * SPAN], U32, align_bytes=LINE)
        s_arrived = const.tile([P, C // PLANES, ROW], U8, align_bytes=LINE)
        nc.vector.memset(s_arrived[:].rearrange("p a n -> p (a n)").bitcast(I32), 0)
        w_scales = const.tile([P, C // PLANES, (LONG + 2) * SPAN], U8, align_bytes=LINE)
        nc.vector.memset(w_scales[:].rearrange("p a n -> p (a n)").bitcast(I32), 0)

        ident = const.tile([P, P], F32, align_bytes=LINE)
        make_identity(nc, ident[:])
        nc.gpsimd.memset(w_codes[:, :, :, SPAN : 2 * SPAN], 0)

        ev_rows, pb_rows, feat_rows = {}, {}, {}

        def pair_rows(matrix, g):
            return matrix[GROUP * g : GROUP * (g + 1)].rearrange("c i n -> (c i) n").rearrange("(p l) n -> p l n", l=LONG)

        def load_rows(matrix, g, name):
            rows = resident.tile([P, LONG, ROW], BF16, name=name, align_bytes=LINE)
            nc.sync.dma_start(out=rows[:], in_=pair_rows(matrix, g))
            return rows

        def load_scales(a):
            for quad in range(QUADRANTS):
                nc.sync.dma_start(
                    out=s_arrived[32 * quad : 32 * quad + 16, a, :].bitcast(I32),
                    in_=W_pie_scales[PLANES * a : PLANES * (a + 1), 4 * quad : 4 * quad + 4, :].bitcast(I32),
                )

        def load_w(g):
            pair = slice(GROUP * g, GROUP * (g + 1))
            nc.sync.dma_start(
                out=w_arrived[:, pair, :].bitcast(I32),
                in_=W_pie_words[pair].rearrange("c p n t -> p c (n t)").bitcast(I32),
            )

        def load_ev(c):
            ev_rows[c] = by_community.tile([P, TILES, ROW], BF16, name="ev_c", align_bytes=LINE)
            nc.sync.dma_start(out=ev_rows[c][:], in_=Ev[c].rearrange("(p r) k -> p r k", r=TILES))

        def load_pb(g):
            pb_rows[g] = load_rows(Pb, g, "pb_g")

        def load_feat(g):
            feat_rows[g] = load_rows(feat, g, "feat_g")

        load_ev(0)
        load_scales(0)
        load_w(0)
        load_ev(1)
        load_pb(0)
        load_ev(2)
        load_ev(3)
        load_w(1)
        load_pb(1)
        load_ev(4)
        load_feat(0)
        load_ev(5)
        load_scales(1)
        load_w(2)
        load_pb(2)
        load_ev(6)
        load_feat(1)
        load_ev(7)
        load_w(3)
        load_pb(3)
        load_feat(2)
        load_feat(3)

        flipped, ev_kfirst, ev_codes, ev_scales, tt, gain_d, factors, out_rows = {}, {}, {}, {}, {}, {}, {}, {}

        def transposes(g, cc):
            ev_words = ev_rows[GROUP * g + cc][:].rearrange("p r k -> p (r k)").bitcast(F32)
            for b in range(BANKS):
                flipped[g, cc, b] = psum_flip.tile([P, FLIPS, P], F32, name="flipped")
                for a in range(FLIPS):
                    r, u = 2 * b + a // 2, a % 2
                    nc.tensor.transpose(
                        flipped[g, cc, b][:, a, :], ev_words[:, WORDS * r + u : WORDS * (r + 1) : 2], ident[:]
                    )

        def copies(g, cc):
            if cc == 0:
                ev_kfirst[g] = work.tile([P, GROUP, ROW * PACK], BF16, name="ev_kfirst", align_bytes=LINE)
            kfirst_words = ev_kfirst[g][:, cc, :].bitcast(F32).rearrange("q (p b a) -> q p b a", b=BANKS, a=FLIPS)
            for b in range(BANKS):
                nc.scalar.copy(out=kfirst_words[:, :, b, :], in_=flipped[g, cc, b][:].rearrange("q a p -> q p a"))

        def quantise(g, cc):
            if cc == 0:
                ev_codes[g] = work.tile([P, GROUP, ROW], U32, name="ev_codes", align_bytes=LINE)
                ev_scales[g] = work.tile([P, GROUP, ROW], U8, name="ev_scales", align_bytes=LINE)
            nc.vector.quantize_mx(
                out=ev_codes[g][:, cc, :].bitcast(FP8X4),
                scales=ev_scales[g][:, cc, :],
                in_=ev_kfirst[g][:, cc, :],
            )

        def reorder_scales(a):
            for half in range(2):
                first = SPAN + LONG // 2 * SPAN * half
                nc.vector.tensor_copy(
                    out=w_scales[:, a, first : first + LONG // 2 * SPAN].rearrange("p (r m) -> p m r", r=LONG // 2),
                    in_=s_arrived[:, a, :].rearrange("p (m h r) -> p h m r", h=2, r=LONG // 2)[:, half],
                )

        def reorder(g, cc):
            nc.vector.tensor_copy(
                out=w_codes[:, g, :, 2 * SPAN * cc : 2 * SPAN * cc + SPAN].bitcast(I32),
                in_=w_arrived[:, GROUP * g + cc, :].bitcast(I32).rearrange("p (m r) -> p r m", r=LONG),
            )

        def passes(g, r):
            tt[g, r] = psum_tt.tile([P, ROW], F32, name="tt")
            for cc in range(GROUP):
                c = GROUP * g + cc
                first = SPAN * cc
                nc.tensor.matmul_mx(
                    out=tt[g, r][:],
                    lhsT=w_codes[:, g, r, first : first + P].bitcast(FP8X4),
                    lhsT_scale=w_scales[4 * (c % PLANES) : P, c // PLANES, SPAN * (r + 1) - first : SPAN * (r + 1) - first + P],
                    rhs=ev_codes[g][:, cc, :].bitcast(FP8X4),
                    rhs_scale=ev_scales[g][:, cc, :],
                    start=(cc == 0),
                    stop=(cc == GROUP - 1),
                )

        def products(g, r):
            if r == 0:
                gain_d[g] = work.tile([P, LONG], F32, name="gain_d", align_bytes=LINE)
            scratch = work.tile([P, ROW], F32, name="scratch", align_bytes=LINE)
            nc.vector.scalar_tensor_tensor(
                out=scratch[:],
                in0=tt[g, r][:],
                scalar=GAIN,
                in1=pb_rows[g][:, r, :],
                op0=MULT,
                op1=MULT,
                accum_out=gain_d[g][:, r : r + 1],
            )

        def make_factors(g):
            factors[g] = work.tile([P, LONG], F32, name="factors", align_bytes=LINE)
            nc.scalar.activation(out=factors[g][:], in_=gain_d[g][:], func=COPY, bias=1.0)
            out_rows[g] = resident.tile([P, LONG, ROW], F32, name="out_g", align_bytes=LINE)

        def scale(g, rows):
            for l in rows:
                nc.scalar.activation(
                    out=out_rows[g][:, l, :], in_=feat_rows[g][:, l, :], func=COPY, scale=factors[g][:, l : l + 1]
                )

        def scale_on_vector(g, rows):
            for l in rows:
                nc.vector.tensor_scalar(
                    out=out_rows[g][:, l, :], in0=feat_rows[g][:, l, :], scalar1=factors[g][:, l : l + 1], scalar2=None, op0=MULT
                )

        def store(queue, g):
            queue.dma_start(out=pair_rows(out, g), in_=out_rows[g][:])

        HALF = LONG // 2
        for half in range(2):
            transposes(0, half)
            copies(0, half)
        reorder_scales(0)
        for cc in range(GROUP):
            reorder(0, cc)
        for cc in range(GROUP):
            quantise(0, cc)
        for g in range(PAIRS):
            more = g + 1 < PAIRS
            for r in range(HALF):
                passes(g, r)
            if g == 0:
                transposes(1, 0)
            if more:
                transposes(g + 1, 1)
            if g > 0:
                make_factors(g - 1)
                scale(g - 1, range(3))
            if g == PAIRS - 1:
                store(nc.scalar, 0)
            if g == 0:
                copies(1, 0)
            if more:
                copies(g + 1, 1)
            for r in range(HALF):
                products(g, r)
            if more:
                if (GROUP * (g + 1)) % PLANES == 0:
                    reorder_scales(GROUP * (g + 1) // PLANES)
                for cc in range(GROUP):
                    reorder(g + 1, cc)
                quantise(g + 1, 0)
            for r in range(HALF, LONG):
                passes(g, r)
            if g + 2 < PAIRS:
                transposes(g + 2, 0)
            for r in range(HALF, HALF + 2):
                products(g, r)
            if more:
                quantise(g + 1, 1)
            for r in range(HALF + 2, LONG):
                products(g, r)
            if g > 0:
                scale(g - 1, range(3, LONG))
                if g == 2:
                    store(nc.sync, 1)
                if g == PAIRS - 1:
                    store(nc.scalar, 2)
            if g + 2 < PAIRS:
                copies(g + 2, 0)
        last = PAIRS - 1
        make_factors(last)
        scale(last, range(3))
        scale_on_vector(last, range(3, LONG))
        store(nc.sync, last)
